import numpy as np
import ml_dtypes


def mxq(x, axis, fmt="e4m3"):
    dtype, down = {"e4m3": (ml_dtypes.float8_e4m3fn, 7), "e5m2": (ml_dtypes.float8_e5m2, 14)}[fmt]
    v = np.moveaxis(np.asarray(x, np.float32).astype(ml_dtypes.bfloat16).astype(np.float64), axis, -1)
    blocks = v.reshape(v.shape[:-1] + (-1, 32))
    amax = np.abs(blocks).max(-1, keepdims=True)
    byte = np.maximum(np.where(amax > 0, np.frexp(amax)[1] - 1 + 127, 0) - down, 1)
    scale = np.exp2(byte - 127.0)
    codes = (blocks / scale).astype(np.float32).astype(dtype).astype(np.float64)
    return np.moveaxis((codes * scale).reshape(v.shape), -1, axis)


WIDE = False


def mx_kscale(k):
    if not WIDE:
        return np.ones(k)
    levels = np.array([30, -30])
    if k % 512:
        return np.exp2(np.random.permutation(np.resize(levels, k // 32))).repeat(32)
    a = np.empty((k // 512, 16))
    for p in range(k // 512):
        a[p, :8] = np.random.permutation(np.resize(levels, 8))
        for g in range(8):
            far = levels[np.abs(levels - a[p, g]) >= 10]
            a[p, g + 8] = far[np.random.randint(len(far))]
    return np.exp2(a.ravel()).repeat(32)


BF16 = ml_dtypes.bfloat16


def bf(x):
    return np.asarray(x, np.float32).astype(BF16)


def f64(x):
    return np.asarray(x).astype(np.float64)


B, S, DIM, H, HD = 4, 128, 2048, 16, 128
E = H * HD


def rope_tables():
    inv_freq = 1.0 / (10000.0 ** (np.arange(0, HD, 2) / HD))
    freqs = np.outer(np.arange(S), inv_freq)
    emb = np.concatenate([freqs, freqs], axis=-1)
    return np.cos(emb)[None, None], np.sin(emb)[None, None]


def rotate_half(x):
    x1, x2 = np.split(x, 2, axis=-1)
    return np.concatenate([-x2, x1], axis=-1)


def setup_inputs():
    s = mx_kscale(DIM)
    cos, sin = rope_tables()
    return {"key_value": bf(np.random.standard_normal((B, S, DIM)) * s),
            "wk": bf(np.random.standard_normal((E, DIM)) / np.sqrt(DIM) / s),
            "bk": bf(np.random.standard_normal(E) * 0.1),
            "wv": bf(np.random.standard_normal((E, DIM)) / np.sqrt(DIM) / s),
            "bv": bf(np.random.standard_normal(E) * 0.1),
            "cos": bf(cos), "sin": bf(sin)}


def reference(key_value, wk, bk, wv, bv, cos, sin):
    xq = mxq(f64(key_value), 2, "e5m2")
    k = (xq @ mxq(f64(wk), 1, "e5m2").T) + f64(bk)
    v = (xq @ mxq(f64(wv), 1, "e5m2").T) + f64(bv)
    k = k.reshape(B, S, H, HD).transpose(0, 2, 1, 3)
    v = v.reshape(B, S, H, HD).transpose(0, 2, 1, 3)
    k = k * f64(cos) + rotate_half(k) * f64(sin)
    return k, v

@@ -1,0 +1,323 @@
+from contextlib import ExitStack
+
+import concourse.mybir as mybir
+from concourse.masks import make_identity
+
+B, S, DIM, H, HD = 4, 128, 2048, 16, 128
+E = H * HD
+FLOPS = 2 * 2 * B * S * DIM * E
+
+F32 = mybir.dt.float32
+BF16 = mybir.dt.bfloat16
+U32 = mybir.dt.uint32
+U8 = mybir.dt.uint8
+FP8X4 = mybir.dt.float8_e5m2_x4
+ADD = mybir.AluOpType.add
+MULT = mybir.AluOpType.mult
+
+P = 128
+N_TILE = 512
+HEADS_PER_TILE = N_TILE // HD
+FT_ORDER = (("k", 0), ("k", 1), ("v", 0), ("k", 2), ("k", 3), ("v", 1), ("v", 2), ("v", 3))
+KHALF_FTS = 2
+RAW_BUFS = 24
+N_WARM = 6
+FILL_NS = 1800
+
+
+def tile_attention_pb_kernel(tc, key_value, wk, bk, wv, bv, cos, sin, out_0, out_1):
+    nc = tc.nc
+    xf = key_value.flatten_outer_dims()
+    n_runs = 2 * len(FT_ORDER)
+
+    with ExitStack() as ctx:
+        const = ctx.enter_context(tc.tile_pool(name="const", bufs=1))
+        rawp = ctx.enter_context(tc.tile_pool(name="rawp", bufs=RAW_BUFS))
+        grp = ctx.enter_context(tc.tile_pool(name="grp", bufs=4))
+        codep = ctx.enter_context(tc.tile_pool(name="codep", bufs=8))
+        kep = ctx.enter_context(tc.tile_pool(name="kep", bufs=2))
+        vep = ctx.enter_context(tc.tile_pool(name="vep", bufs=6))
+        tps = ctx.enter_context(tc.psum_pool(name="tps", bufs=4))
+        accp = ctx.enter_context(tc.psum_pool(name="accp", bufs=4))
+        ctx.enter_context(tc.manual_schedule())
+
+        warm = const.tile([P, N_TILE], BF16, name="warm")
+        nc.vector.memset(warm[:], 0.0)
+        brows = const.tile([P, N_TILE], BF16, name="brows")
+        nc.vector.memset(brows[:], 0.0)
+        ident = const.tile([P, P], F32, name="ident")
+        make_identity(nc, ident[:])
+        identb = const.tile([P, P], BF16, name="identb")
+        make_identity(nc, identb[:])
+
+        cosb = const.tile([P, HD], BF16, name="cosb")
+        sinb = const.tile([P, HD], BF16, name="sinb")
+        nc.scalar.dma_start(out=sinb[:], in_=sin.flatten_outer_dims())
+        nc.scalar.dma_start(out=cosb[:], in_=cos.flatten_outer_dims())
+        nc.scalar.dma_start(out=brows[0:4, :], in_=bk.rearrange("(f n) -> f n", n=N_TILE))
+        nc.scalar.dma_start(out=brows[4:8, :], in_=bv.rearrange("(f n) -> f n", n=N_TILE))
+        scratch = const.tile([P, 1], F32, name="scratch")
+        nc.scalar.copy(out=scratch[:], in_=warm[:, 0:1])
+
+        xraw = []
+        for m in range(B):
+            xt = rawp.tile([P, DIM], BF16, name="raw", tag="raw")
+            nc.sync.dma_start(out=xt[:], in_=xf[m * P:(m + 1) * P, :])
+            xraw.append(xt)
+
+        wtiles = {}
+
+        def load_ft(i):
+            which, f = FT_ORDER[i]
+            src = wk if which == "k" else wv
+            tiles = []
+            if i < KHALF_FTS:
+                for kh in range(2):
+                    for pair in range(2):
+                        wt = rawp.tile([P, DIM], BF16, name="raw", tag="raw")
+                        r0 = f * N_TILE + pair * 2 * P
+                        nc.sync.dma_start(
+                            out=wt[:].rearrange("p (r k) -> p r k", r=2),
+                            in_=src[r0:r0 + 2 * P, kh * 1024:(kh + 1) * 1024].rearrange("(r p) k -> p r k", p=P),
+                        )
+                        tiles.append(wt)
+            else:
+                for rb in range(4):
+                    wt = rawp.tile([P, DIM], BF16, name="raw", tag="raw")
+                    r0 = f * N_TILE + rb * P
+                    nc.sync.dma_start(out=wt[:], in_=src[r0:r0 + P, :])
+                    tiles.append(wt)
+            wtiles[i] = tiles
+
+        def w_words(i, rb, c):
+            if i < KHALF_FTS:
+                wt = wtiles[i][(c // 2) * 2 + rb // 2]
+                base = (rb % 2) * 512 + (c % 2) * 256
+            else:
+                wt = wtiles[i][rb]
+                base = c * 256
+            return wt[:].bitcast(F32), base
+
+        for i in range(5):
+            load_ft(i)
+
+        nsin = const.tile([P, HD], BF16, name="nsin")
+        nc.vector.tensor_scalar(out=nsin[:, 0:64], in0=sinb[:, 0:64], scalar1=-1.0, scalar2=None, op0=MULT)
+        nc.vector.tensor_copy(out=nsin[:, 64:128], in_=sinb[:, 64:128])
+
+        def word_rows(g, lo, hi):
+            return g[:].bitcast(F32).rearrange("p (r u) -> p r u", u=2)[:, lo:hi, :]
+
+        def bank_out(bank):
+            return bank[:].rearrange("p u r -> p r u")
+
+        bias = {}
+
+        def bias_mm(i, engine):
+            which, f = FT_ORDER[i]
+            row = f if which == "k" else 4 + f
+            ps = accp.tile([P, N_TILE], F32, name="acc", tag="acc")
+            nc.tensor.matmul(out=ps[:], lhsT=identb[:, row:row + 1].to_broadcast([P, P]), rhs=brows[:], start=True, stop=True)
+            bt = const.tile([P, N_TILE], BF16, name="bias%d" % i)
+            if engine == "s":
+                nc.scalar.copy(out=bt[:], in_=ps[:])
+            else:
+                nc.vector.tensor_copy(out=bt[:], in_=ps[:])
+            bias[i] = bt
+
+        xg = {}
+        xcodes = {}
+        xscales = {}
+
+        def t_run_x(ms):
+            for m in ms:
+                g = grp.tile([P, DIM], BF16, name="grouped", tag="grouped", align_bytes=64)
+                words = xraw[m][:].bitcast(F32)
+                for ch in range(2):
+                    bank = tps.tile([P, 2, 256], F32, name="tp", tag="tp")
+                    for cl in range(2):
+                        c = 2 * ch + cl
+                        for u in range(2):
+                            nc.tensor.transpose(bank[:, u, cl * P:(cl + 1) * P], words[:, c * 256 + u:(c + 1) * 256:2], ident[:])
+                    if ch == 0:
+                        nc.scalar.copy(out=word_rows(g, 0, 256), in_=bank_out(bank))
+                    else:
+                        nc.vector.tensor_copy(out=word_rows(g, 256, 512), in_=bank_out(bank))
+                xg[m] = g
+
+        def quant_x(m):
+            xc = const.tile([P, N_TILE], U32, name="xcodes%d" % m, align_bytes=64)
+            xs = const.tile([P, N_TILE], U8, name="xscales%d" % m, align_bytes=64)
+            nc.vector.quantize_mx(out=xc[:].bitcast(FP8X4), scales=xs[:], in_=xg[m][:])
+            xcodes[m] = xc
+            xscales[m] = xs
+
+        wg = {}
+        wcodes = {}
+        wscales = {}
+
+        def t_run_w(r):
+            i, kh = divmod(r, 2)
+            g0 = grp.tile([P, DIM], BF16, name="grouped", tag="grouped", align_bytes=64)
+            g1 = grp.tile([P, DIM], BF16, name="grouped", tag="grouped", align_bytes=64)
+            gs = (g0, g1)
+            for pair in range(2):
+                for cl in range(2):
+                    c = 2 * kh + cl
+                    bank = tps.tile([P, 2, 256], F32, name="tp", tag="tp")
+                    for rl in range(2):
+                        words, base = w_words(i, 2 * pair + rl, c)
+                        for u in range(2):
+                            nc.tensor.transpose(bank[:, u, rl * P:(rl + 1) * P], words[:, base + u:base + 256:2], ident[:])
+                    nc.scalar.copy(out=word_rows(gs[cl], pair * 256, (pair + 1) * 256), in_=bank_out(bank))
+            wg[r] = gs
+
+        def quant_w(r):
+            i, kh = divmod(r, 2)
+            for cl in range(2):
+                wc = codep.tile([P, N_TILE], U32, name="wcodes", tag="wcodes", align_bytes=64)
+                ws = codep.tile([P, N_TILE], U8, name="wscales", tag="wscales", align_bytes=64)
+                nc.vector.quantize_mx(out=wc[:].bitcast(FP8X4), scales=ws[:], in_=wg[r][cl][:])
+                wcodes[(i, 2 * kh + cl)] = wc
+                wscales[(i, 2 * kh + cl)] = ws
+
+        accs = {}
+
+        def m_run(r):
+            i, kh = divmod(r, 2)
+            if kh == 0:
+                tiles = []
+                for m in range(B):
+                    acc = accp.tile([P, N_TILE], F32, name="acc", tag="acc")
+                    tiles.append(acc)
+                accs[i] = tiles
+            for m in range(B):
+                for cl in range(2):
+                    c = 2 * kh + cl
+                    nc.tensor.matmul_mx(
+                        out=accs[i][m][:],
+                        lhsT=xcodes[m][:, c * P:(c + 1) * P].bitcast(FP8X4),
+                        lhsT_scale=xscales[m][:, c * P:(c + 1) * P],
+                        rhs=wcodes[(i, c)][:].bitcast(FP8X4),
+                        rhs_scale=wscales[(i, c)][:],
+                        start=(c == 0),
+                        stop=(c == 3),
+                    )
+
+        fills = []
+        fill_state = {"next": 0}
+
+        def emit_fills(budget):
+            spent = 0
+            while fill_state["next"] < len(fills):
+                cost, fn = fills[fill_state["next"]]
+                if spent + cost > budget:
+                    break
+                fn()
+                spent += cost
+                fill_state["next"] += 1
+
+        def heads(ap):
+            return ap.rearrange("p m (h d) -> p (m h) d", d=HD)
+
+        def read_k(i):
+            f = FT_ORDER[i][1]
+            t = kep.tile([P, B, N_TILE], F32, name="t", tag="t")
+            for m in range(B):
+                nc.vector.tensor_tensor(out=t[:, m, :], in0=accs[i][m][:], in1=bias[i][:], op=ADD)
+            hold = {}
+            nh = 2 * HEADS_PER_TILE
+
+            def mul_cos(j):
+                if j == 0:
+                    a = kep.tile([P, B, N_TILE], F32, name="a", tag="a")
+                    hold["a"] = a
+                nc.vector.tensor_tensor(
+                    out=heads(hold["a"][:, 2 * j:2 * j + 2, :]),
+                    in0=heads(t[:, 2 * j:2 * j + 2, :]),
+                    in1=cosb[:].unsqueeze(1).to_broadcast([P, nh, HD]),
+                    op=MULT,
+                )
+
+            def mul_sin(j, half):
+                if j == 0 and half == 0:
+                    b = kep.tile([P, B, N_TILE], F32, name="b", tag="b", bufs=1)
+                    hold["b"] = b
+                dst = slice(64 * half, 64 * half + 64)
+                src = slice(64 - 64 * half, 128 - 64 * half)
+                nc.vector.tensor_tensor(
+                    out=heads(hold["b"][:, 2 * j:2 * j + 2, :])[:, :, dst],
+                    in0=heads(t[:, 2 * j:2 * j + 2, :])[:, :, src],
+                    in1=nsin[:, dst].unsqueeze(1).to_broadcast([P, nh, 64]),
+                    op=MULT,
+                )
+
+            def add_store(j):
+                av = hold["a"][:, 2 * j:2 * j + 2, :]
+                nc.vector.tensor_tensor(out=av, in0=av, in1=hold["b"][:, 2 * j:2 * j + 2, :], op=ADD)
+                for m in (2 * j, 2 * j + 1):
+                    nc.sync.dma_start(
+                        out=out_0[m, f * HEADS_PER_TILE:(f + 1) * HEADS_PER_TILE, :, :].rearrange("h s d -> s h d"),
+                        in_=hold["a"][:, m, :].rearrange("p (h d) -> p h d", d=HD),
+                    )
+
+            fills.append((870, lambda: mul_cos(0)))
+            fills.append((870, lambda: mul_cos(1)))
+            fills.append((440, lambda: mul_sin(0, 0)))
+            fills.append((440, lambda: mul_sin(0, 1)))
+            fills.append((440, lambda: mul_sin(1, 0)))
+            fills.append((440, lambda: mul_sin(1, 1)))
+            fills.append((870, lambda: add_store(0)))
+            fills.append((870, lambda: add_store(1)))
+
+        def read_v(i):
+            f = FT_ORDER[i][1]
+            for m in range(B):
+                vout = vep.tile([P, N_TILE], F32, name="vout", tag="vout")
+                nc.vector.tensor_tensor(out=vout[:], in0=accs[i][m][:], in1=bias[i][:], op=ADD)
+                nc.sync.dma_start(
+                    out=out_1[m, f * HEADS_PER_TILE:(f + 1) * HEADS_PER_TILE, :, :].rearrange("h s d -> s h d"),
+                    in_=vout[:].rearrange("p (h d) -> p h d", d=HD),
+                )
+
+        wps = accp.tile([P, N_TILE], F32, name="acc", tag="acc")
+        for n in range(N_WARM):
+            nc.tensor.matmul(out=wps[:], lhsT=warm[:, 0:P], rhs=warm[:], start=True, stop=True)
+
+        t_run_x((0, 1))
+        bias_mm(0, "s")
+        bias_mm(1, "v")
+        quant_x(0)
+        quant_x(1)
+        t_run_x((2, 3))
+        bias_mm(2, "s")
+        bias_mm(3, "v")
+        quant_x(2)
+        quant_x(3)
+        load_ft(5)
+        t_run_w(0)
+        bias_mm(4, "s")
+        bias_mm(5, "v")
+        quant_w(0)
+
+        for r in range(n_runs):
+            if r + 1 < n_runs:
+                t_run_w(r + 1)
+            if r == 0:
+                bias_mm(6, "s")
+                bias_mm(7, "v")
+            if r == 0:
+                load_ft(6)
+            if r == 2:
+                load_ft(7)
+            emit_fills(FILL_NS if r < n_runs - 2 else 1000000)
+            if r + 1 < n_runs:
+                quant_w(r + 1)
+            m_run(r)
+            if r % 2 == 1:
+                i = r // 2
+                if FT_ORDER[i][0] == "k":
+                    read_k(i)
+                else:
+                    read_v(i)
+        emit_fills(1000000)

@@ -20,9 +20,11 @@ N_TILE = 512
 HEADS_PER_TILE = N_TILE // HD
 FT_ORDER = (("k", 0), ("k", 1), ("v", 0), ("k", 2), ("k", 3), ("v", 1), ("v", 2), ("v", 3))
 KHALF_FTS = 2
-RAW_BUFS = 24
+RAW_BUFS = 20
 N_WARM = 6
-FILL_NS = 1800
+FILL_NS = 1320
+REORD_RBS = (0, 1, 2)
+FIRST_REORD_RUN = 3
 
 
 def tile_attention_pb_kernel(tc, key_value, wk, bk, wv, bv, cos, sin, out_0, out_1):
@@ -33,12 +35,14 @@ def tile_attention_pb_kernel(tc, key_value, wk, bk, wv, bv, cos, sin, out_0, out
     with ExitStack() as ctx:
         const = ctx.enter_context(tc.tile_pool(name="const", bufs=1))
         rawp = ctx.enter_context(tc.tile_pool(name="rawp", bufs=RAW_BUFS))
-        grp = ctx.enter_context(tc.tile_pool(name="grp", bufs=4))
-        codep = ctx.enter_context(tc.tile_pool(name="codep", bufs=8))
-        kep = ctx.enter_context(tc.tile_pool(name="kep", bufs=2))
+        rop = ctx.enter_context(tc.tile_pool(name="rop", bufs=9))
+        grp = ctx.enter_context(tc.tile_pool(name="grp", bufs=3))
+        codep = ctx.enter_context(tc.tile_pool(name="codep", bufs=6))
+        kep = ctx.enter_context(tc.tile_pool(name="kep", bufs=3))
         vep = ctx.enter_context(tc.tile_pool(name="vep", bufs=6))
         tps = ctx.enter_context(tc.psum_pool(name="tps", bufs=4))
-        accp = ctx.enter_context(tc.psum_pool(name="accp", bufs=4))
+        accp = ctx.enter_context(tc.psum_pool(name="accp", bufs=3))
+        tabp = ctx.enter_context(tc.psum_pool(name="tabp", bufs=1))
         ctx.enter_context(tc.manual_schedule())
 
         warm = const.tile([P, N_TILE], BF16, name="warm")
@@ -89,16 +93,17 @@ def tile_attention_pb_kernel(tc, key_value, wk, bk, wv, bv, cos, sin, out_0, out
                     tiles.append(wt)
             wtiles[i] = tiles
 
-        def w_words(i, rb, c):
+        def run_words(r, rb):
+            i, kh = divmod(r, 2)
             if i < KHALF_FTS:
-                wt = wtiles[i][(c // 2) * 2 + rb // 2]
-                base = (rb % 2) * 512 + (c % 2) * 256
+                wt = wtiles[i][kh * 2 + rb // 2]
+                base = (rb % 2) * 512
             else:
                 wt = wtiles[i][rb]
-                base = c * 256
-            return wt[:].bitcast(F32), base
+                base = kh * 512
+            return wt[:].bitcast(F32)[:, base:base + 512]
 
-        for i in range(5):
+        for i in range(4):
             load_ft(i)
 
         nsin = const.tile([P, HD], BF16, name="nsin")
@@ -129,152 +134,149 @@ def tile_attention_pb_kernel(tc, key_value, wk, bk, wv, bv, cos, sin, out_0, out
         xcodes = {}
         xscales = {}
 
-        def t_run_x(ms):
-            for m in ms:
-                g = grp.tile([P, DIM], BF16, name="grouped", tag="grouped", align_bytes=64)
-                words = xraw[m][:].bitcast(F32)
+        def t_run_x(half):
+            g = grp.tile([P, 2 * DIM], BF16, name="grouped", tag="grouped", align_bytes=64)
+            for ml in range(2):
+                words = xraw[2 * half + ml][:].bitcast(F32)
                 for ch in range(2):
                     bank = tps.tile([P, 2, 256], F32, name="tp", tag="tp")
                     for cl in range(2):
                         c = 2 * ch + cl
                         for u in range(2):
                             nc.tensor.transpose(bank[:, u, cl * P:(cl + 1) * P], words[:, c * 256 + u:(c + 1) * 256:2], ident[:])
+                    lo = ml * 512 + ch * 256
                     if ch == 0:
-                        nc.scalar.copy(out=word_rows(g, 0, 256), in_=bank_out(bank))
+                        nc.scalar.copy(out=word_rows(g, lo, lo + 256), in_=bank_out(bank))
                     else:
-                        nc.vector.tensor_copy(out=word_rows(g, 256, 512), in_=bank_out(bank))
-                xg[m] = g
+                        nc.vector.tensor_copy(out=word_rows(g, lo, lo + 256), in_=bank_out(bank))
+            xg[half] = g
 
-        def quant_x(m):
-            xc = const.tile([P, N_TILE], U32, name="xcodes%d" % m, align_bytes=64)
-            xs = const.tile([P, N_TILE], U8, name="xscales%d" % m, align_bytes=64)
-            nc.vector.quantize_mx(out=xc[:].bitcast(FP8X4), scales=xs[:], in_=xg[m][:])
-            xcodes[m] = xc
-            xscales[m] = xs
+        def quant_x(half):
+            xc = const.tile([P, 2 * N_TILE], U32, name="xcodes%d" % half, align_bytes=64)
+            xs = const.tile([P, 2 * N_TILE], U8, name="xscales%d" % half, align_bytes=64)
+            nc.vector.quantize_mx(out=xc[:].bitcast(FP8X4), scales=xs[:], in_=xg[half][:])
+            xcodes[half] = xc
+            xscales[half] = xs
 
         wg = {}
         wcodes = {}
         wscales = {}
+        reord = {}
+
+        def reorder_run(r):
+            for rb in REORD_RBS:
+                ro = rop.tile([P, 512], F32, name="ro", tag="ro")
+                nc.scalar.copy(
+                    out=ro[:].rearrange("p (c u q) -> p c u q", c=2, u=2),
+                    in_=run_words(r, rb).rearrange("p (c q u) -> p c u q", c=2, u=2),
+                )
+                reord[(r, rb)] = ro
 
         def t_run_w(r):
-            i, kh = divmod(r, 2)
-            g0 = grp.tile([P, DIM], BF16, name="grouped", tag="grouped", align_bytes=64)
-            g1 = grp.tile([P, DIM], BF16, name="grouped", tag="grouped", align_bytes=64)
-            gs = (g0, g1)
+            g = grp.tile([P, 2 * DIM], BF16, name="grouped", tag="grouped", align_bytes=64)
             for pair in range(2):
                 for cl in range(2):
-                    c = 2 * kh + cl
                     bank = tps.tile([P, 2, 256], F32, name="tp", tag="tp")
                     for rl in range(2):
-                        words, base = w_words(i, 2 * pair + rl, c)
+                        rb = 2 * pair + rl
                         for u in range(2):
-                            nc.tensor.transpose(bank[:, u, rl * P:(rl + 1) * P], words[:, base + u:base + 256:2], ident[:])
-                    nc.scalar.copy(out=word_rows(gs[cl], pair * 256, (pair + 1) * 256), in_=bank_out(bank))
-            wg[r] = gs
+                            if (r, rb) in reord:
+                                src = reord[(r, rb)][:, cl * 256 + u * P:cl * 256 + (u + 1) * P]
+                            else:
+                                src = run_words(r, rb)[:, cl * 256 + u:(cl + 1) * 256:2]
+                            nc.tensor.transpose(bank[:, u, rl * P:(rl + 1) * P], src, ident[:])
+                    lo = cl * 512 + pair * 256
+                    nc.scalar.copy(out=word_rows(g, lo, lo + 256), in_=bank_out(bank))
+            wg[r] = g
 
         def quant_w(r):
-            i, kh = divmod(r, 2)
-            for cl in range(2):
-                wc = codep.tile([P, N_TILE], U32, name="wcodes", tag="wcodes", align_bytes=64)
-                ws = codep.tile([P, N_TILE], U8, name="wscales", tag="wscales", align_bytes=64)
-                nc.vector.quantize_mx(out=wc[:].bitcast(FP8X4), scales=ws[:], in_=wg[r][cl][:])
-                wcodes[(i, 2 * kh + cl)] = wc
-                wscales[(i, 2 * kh + cl)] = ws
+            wc = codep.tile([P, 2 * N_TILE], U32, name="wcodes", tag="wcodes", align_bytes=64)
+            ws = codep.tile([P, 2 * N_TILE], U8, name="wscales", tag="wscales", align_bytes=64)
+            nc.vector.quantize_mx(out=wc[:].bitcast(FP8X4), scales=ws[:], in_=wg[r][:])
+            wcodes[r] = wc
+            wscales[r] = ws
 
         accs = {}
 
-        def m_run(r):
-            i, kh = divmod(r, 2)
-            if kh == 0:
-                tiles = []
-                for m in range(B):
-                    acc = accp.tile([P, N_TILE], F32, name="acc", tag="acc")
-                    tiles.append(acc)
-                accs[i] = tiles
-            for m in range(B):
-                for cl in range(2):
-                    c = 2 * kh + cl
-                    nc.tensor.matmul_mx(
-                        out=accs[i][m][:],
-                        lhsT=xcodes[m][:, c * P:(c + 1) * P].bitcast(FP8X4),
-                        lhsT_scale=xscales[m][:, c * P:(c + 1) * P],
-                        rhs=wcodes[(i, c)][:].bitcast(FP8X4),
-                        rhs_scale=wscales[(i, c)][:],
-                        start=(c == 0),
-                        stop=(c == 3),
-                    )
+        def m_group(i, m):
+            acc = accp.tile([P, N_TILE], F32, name="acc", tag="acc")
+            for c in range(4):
+                r = 2 * i + c // 2
+                wcol = slice((c % 2) * N_TILE, (c % 2 + 1) * N_TILE)
+                xcol = slice((m % 2) * N_TILE + c * P, (m % 2) * N_TILE + (c + 1) * P)
+                nc.tensor.matmul_mx(
+                    out=acc[:],
+                    lhsT=xcodes[m // 2][:, xcol].bitcast(FP8X4),
+                    lhsT_scale=xscales[m // 2][:, xcol],
+                    rhs=wcodes[r][:, wcol].bitcast(FP8X4),
+                    rhs_scale=wscales[r][:, wcol],
+                    start=(c == 0),
+                    stop=(c == 3),
+                )
+            accs[(i, m)] = acc
 
         fills = []
-        fill_state = {"next": 0}
+        fill_state = {"next": 0, "credit": 0}
 
         def emit_fills(budget):
-            spent = 0
+            fill_state["credit"] = min(fill_state["credit"] + budget, 2 * budget)
             while fill_state["next"] < len(fills):
                 cost, fn = fills[fill_state["next"]]
-                if spent + cost > budget:
+                if cost > fill_state["credit"]:
                     break
                 fn()
-                spent += cost
+                fill_state["credit"] -= cost
                 fill_state["next"] += 1
 
         def heads(ap):
             return ap.rearrange("p m (h d) -> p (m h) d", d=HD)
 
-        def read_k(i):
-            f = FT_ORDER[i][1]
-            t = kep.tile([P, B, N_TILE], F32, name="t", tag="t")
-            for m in range(B):
-                nc.vector.tensor_tensor(out=t[:, m, :], in0=accs[i][m][:], in1=bias[i][:], op=ADD)
-            hold = {}
-            nh = 2 * HEADS_PER_TILE
+        tab = tabp.tile([P, 2, HD], F32, name="tab")
+        nh = 2 * HEADS_PER_TILE
 
-            def mul_cos(j):
-                if j == 0:
-                    a = kep.tile([P, B, N_TILE], F32, name="a", tag="a")
-                    hold["a"] = a
+        def read_k(i, ms):
+            f = FT_ORDER[i][1]
+            t = kep.tile([P, 2, N_TILE], F32, name="t", tag="t")
+            for ml in range(2):
+                nc.vector.tensor_tensor(out=t[:, ml, :], in0=accs[(i, ms[ml])][:], in1=bias[i][:], op=ADD)
+            hold = {}
+
+            def mul_cos():
+                a = kep.tile([P, 2, N_TILE], F32, name="a", tag="a")
+                hold["a"] = a
                 nc.vector.tensor_tensor(
-                    out=heads(hold["a"][:, 2 * j:2 * j + 2, :]),
-                    in0=heads(t[:, 2 * j:2 * j + 2, :]),
-                    in1=cosb[:].unsqueeze(1).to_broadcast([P, nh, HD]),
-                    op=MULT,
+                    out=heads(a[:]), in0=heads(t[:]), in1=tab[:, 0, :].unsqueeze(1).to_broadcast([P, nh, HD]), op=MULT
                 )
 
-            def mul_sin(j, half):
-                if j == 0 and half == 0:
-                    b = kep.tile([P, B, N_TILE], F32, name="b", tag="b", bufs=1)
+            def mul_sin(half):
+                if half == 0:
+                    b = kep.tile([P, 2, N_TILE], F32, name="b", tag="b")
                     hold["b"] = b
                 dst = slice(64 * half, 64 * half + 64)
                 src = slice(64 - 64 * half, 128 - 64 * half)
                 nc.vector.tensor_tensor(
-                    out=heads(hold["b"][:, 2 * j:2 * j + 2, :])[:, :, dst],
-                    in0=heads(t[:, 2 * j:2 * j + 2, :])[:, :, src],
-                    in1=nsin[:, dst].unsqueeze(1).to_broadcast([P, nh, 64]),
+                    out=heads(hold["b"][:])[:, :, dst],
+                    in0=heads(t[:])[:, :, src],
+                    in1=tab[:, 1, dst].unsqueeze(1).to_broadcast([P, nh, 64]),
                     op=MULT,
                 )
+                if half == 1:
+                    for ml in range(2):
+                        nc.gpsimd.tensor_tensor(out=hold["a"][:, ml, :], in0=hold["a"][:, ml, :], in1=hold["b"][:, ml, :], op=ADD)
+                        nc.sync.dma_start(
+                            out=out_0[ms[ml], f * HEADS_PER_TILE:(f + 1) * HEADS_PER_TILE, :, :].rearrange("h s d -> s h d"),
+                            in_=hold["a"][:, ml, :].rearrange("p (h d) -> p h d", d=HD),
+                        )
 
-            def add_store(j):
-                av = hold["a"][:, 2 * j:2 * j + 2, :]
-                nc.vector.tensor_tensor(out=av, in0=av, in1=hold["b"][:, 2 * j:2 * j + 2, :], op=ADD)
-                for m in (2 * j, 2 * j + 1):
-                    nc.sync.dma_start(
-                        out=out_0[m, f * HEADS_PER_TILE:(f + 1) * HEADS_PER_TILE, :, :].rearrange("h s d -> s h d"),
-                        in_=hold["a"][:, m, :].rearrange("p (h d) -> p h d", d=HD),
-                    )
+            fills.append((870, mul_cos))
+            fills.append((440, lambda: mul_sin(0)))
+            fills.append((440, lambda: mul_sin(1)))
 
-            fills.append((870, lambda: mul_cos(0)))
-            fills.append((870, lambda: mul_cos(1)))
-            fills.append((440, lambda: mul_sin(0, 0)))
-            fills.append((440, lambda: mul_sin(0, 1)))
-            fills.append((440, lambda: mul_sin(1, 0)))
-            fills.append((440, lambda: mul_sin(1, 1)))
-            fills.append((870, lambda: add_store(0)))
-            fills.append((870, lambda: add_store(1)))
-
-        def read_v(i):
+        def read_v(i, ms):
             f = FT_ORDER[i][1]
-            for m in range(B):
+            for m in ms:
                 vout = vep.tile([P, N_TILE], F32, name="vout", tag="vout")
-                nc.vector.tensor_tensor(out=vout[:], in0=accs[i][m][:], in1=bias[i][:], op=ADD)
+                nc.vector.tensor_tensor(out=vout[:], in0=accs[(i, m)][:], in1=bias[i][:], op=ADD)
                 nc.sync.dma_start(
                     out=out_1[m, f * HEADS_PER_TILE:(f + 1) * HEADS_PER_TILE, :, :].rearrange("h s d -> s h d"),
                     in_=vout[:].rearrange("p (h d) -> p h d", d=HD),
@@ -284,40 +286,45 @@ def tile_attention_pb_kernel(tc, key_value, wk, bk, wv, bv, cos, sin, out_0, out
         for n in range(N_WARM):
             nc.tensor.matmul(out=wps[:], lhsT=warm[:, 0:P], rhs=warm[:], start=True, stop=True)
 
-        t_run_x((0, 1))
+        t_run_x(0)
         bias_mm(0, "s")
         bias_mm(1, "v")
         quant_x(0)
-        quant_x(1)
-        t_run_x((2, 3))
+        t_run_x(1)
         bias_mm(2, "s")
         bias_mm(3, "v")
-        quant_x(2)
-        quant_x(3)
-        load_ft(5)
+        nc.tensor.matmul(out=tab[:, 0, :], lhsT=identb[:], rhs=cosb[:], start=True, stop=True)
+        nc.tensor.matmul(out=tab[:, 1, :], lhsT=identb[:], rhs=nsin[:], start=True, stop=True)
+        quant_x(1)
+        load_ft(4)
         t_run_w(0)
         bias_mm(4, "s")
         bias_mm(5, "v")
         quant_w(0)
+        t_run_w(1)
+        bias_mm(6, "s")
+        bias_mm(7, "v")
+        quant_w(1)
+        load_ft(5)
 
-        for r in range(n_runs):
-            if r + 1 < n_runs:
-                t_run_w(r + 1)
-            if r == 0:
-                bias_mm(6, "s")
-                bias_mm(7, "v")
-            if r == 0:
+        for p in range(n_runs):
+            if p + 2 < n_runs:
+                t_run_w(p + 2)
+            if FIRST_REORD_RUN <= p + 3 < n_runs:
+                reorder_run(p + 3)
+            if p == 1:
                 load_ft(6)
-            if r == 2:
+            if p == 3:
                 load_ft(7)
-            emit_fills(FILL_NS if r < n_runs - 2 else 1000000)
-            if r + 1 < n_runs:
-                quant_w(r + 1)
-            m_run(r)
-            if r % 2 == 1:
-                i = r // 2
-                if FT_ORDER[i][0] == "k":
-                    read_k(i)
-                else:
-                    read_v(i)
+            emit_fills(FILL_NS if p < n_runs - 3 else 1000000)
+            if p + 2 < n_runs:
+                quant_w(p + 2)
+            i = p // 2
+            ms = (2 * (p % 2), 2 * (p % 2) + 1)
+            for m in ms:
+                m_group(i, m)
+            if FT_ORDER[i][0] == "k":
+                read_k(i, ms)
+            else:
+                read_v(i, ms)
         emit_fills(1000000)

@@ -22,8 +22,8 @@ FT_ORDER = (("k", 0), ("k", 1), ("v", 0), ("k", 2), ("k", 3), ("v", 1), ("v", 2)
 KHALF_FTS = 2
 RAW_BUFS = 20
 N_WARM = 6
-FILL_NS = 1320
-REORD_RBS = (0, 1, 2)
+FILL_NS = 1600
+REORD_RBS = (0, 1)
 FIRST_REORD_RUN = 3
 
 
@@ -35,14 +35,13 @@ def tile_attention_pb_kernel(tc, key_value, wk, bk, wv, bv, cos, sin, out_0, out
     with ExitStack() as ctx:
         const = ctx.enter_context(tc.tile_pool(name="const", bufs=1))
         rawp = ctx.enter_context(tc.tile_pool(name="rawp", bufs=RAW_BUFS))
-        rop = ctx.enter_context(tc.tile_pool(name="rop", bufs=9))
+        rop = ctx.enter_context(tc.tile_pool(name="rop", bufs=6))
         grp = ctx.enter_context(tc.tile_pool(name="grp", bufs=3))
         codep = ctx.enter_context(tc.tile_pool(name="codep", bufs=6))
         kep = ctx.enter_context(tc.tile_pool(name="kep", bufs=3))
         vep = ctx.enter_context(tc.tile_pool(name="vep", bufs=6))
         tps = ctx.enter_context(tc.psum_pool(name="tps", bufs=4))
-        accp = ctx.enter_context(tc.psum_pool(name="accp", bufs=3))
-        tabp = ctx.enter_context(tc.psum_pool(name="tabp", bufs=1))
+        accp = ctx.enter_context(tc.psum_pool(name="accp", bufs=4))
         ctx.enter_context(tc.manual_schedule())
 
         warm = const.tile([P, N_TILE], BF16, name="warm")
@@ -167,8 +166,8 @@ def tile_attention_pb_kernel(tc, key_value, wk, bk, wv, bv, cos, sin, out_0, out
             for rb in REORD_RBS:
                 ro = rop.tile([P, 512], F32, name="ro", tag="ro")
                 nc.scalar.copy(
-                    out=ro[:].rearrange("p (c u q) -> p c u q", c=2, u=2),
-                    in_=run_words(r, rb).rearrange("p (c q u) -> p c u q", c=2, u=2),
+                    out=ro[:].rearrange("p (c u q) -> p c q u", c=2, u=2),
+                    in_=run_words(r, rb).rearrange("p (c q u) -> p c q u", c=2, u=2),
                 )
                 reord[(r, rb)] = ro
 
@@ -231,22 +230,13 @@ def tile_attention_pb_kernel(tc, key_value, wk, bk, wv, bv, cos, sin, out_0, out
         def heads(ap):
             return ap.rearrange("p m (h d) -> p (m h) d", d=HD)
 
-        tab = tabp.tile([P, 2, HD], F32, name="tab")
-        nh = 2 * HEADS_PER_TILE
-
         def read_k(i, ms):
             f = FT_ORDER[i][1]
-            t = kep.tile([P, 2, N_TILE], F32, name="t", tag="t")
+            t = kep.tile([P, 2, N_TILE], F32, name="t", tag="t", bufs=4)
             for ml in range(2):
                 nc.vector.tensor_tensor(out=t[:, ml, :], in0=accs[(i, ms[ml])][:], in1=bias[i][:], op=ADD)
             hold = {}
-
-            def mul_cos():
-                a = kep.tile([P, 2, N_TILE], F32, name="a", tag="a")
-                hold["a"] = a
-                nc.vector.tensor_tensor(
-                    out=heads(a[:]), in0=heads(t[:]), in1=tab[:, 0, :].unsqueeze(1).to_broadcast([P, nh, HD]), op=MULT
-                )
+            nh = 2 * HEADS_PER_TILE
 
             def mul_sin(half):
                 if half == 0:
@@ -257,20 +247,34 @@ def tile_attention_pb_kernel(tc, key_value, wk, bk, wv, bv, cos, sin, out_0, out
                 nc.vector.tensor_tensor(
                     out=heads(hold["b"][:])[:, :, dst],
                     in0=heads(t[:])[:, :, src],
-                    in1=tab[:, 1, dst].unsqueeze(1).to_broadcast([P, nh, 64]),
+                    in1=nsin[:, dst].unsqueeze(1).to_broadcast([P, nh, 64]),
                     op=MULT,
                 )
-                if half == 1:
-                    for ml in range(2):
-                        nc.gpsimd.tensor_tensor(out=hold["a"][:, ml, :], in0=hold["a"][:, ml, :], in1=hold["b"][:, ml, :], op=ADD)
-                        nc.sync.dma_start(
-                            out=out_0[ms[ml], f * HEADS_PER_TILE:(f + 1) * HEADS_PER_TILE, :, :].rearrange("h s d -> s h d"),
-                            in_=hold["a"][:, ml, :].rearrange("p (h d) -> p h d", d=HD),
-                        )
 
-            fills.append((870, mul_cos))
+            def mul_cos(ml):
+                if ml == 0:
+                    a = kep.tile([P, 2, N_TILE], F32, name="a", tag="a")
+                    hold["a"] = a
+                nc.vector.tensor_tensor(
+                    out=hold["a"][:, ml, :].rearrange("p (h d) -> p h d", d=HD),
+                    in0=t[:, ml, :].rearrange("p (h d) -> p h d", d=HD),
+                    in1=cosb[:].unsqueeze(1).to_broadcast([P, HEADS_PER_TILE, HD]),
+                    op=MULT,
+                )
+
+            def add_store(ml):
+                nc.vector.tensor_tensor(out=hold["a"][:, ml, :], in0=hold["a"][:, ml, :], in1=hold["b"][:, ml, :], op=ADD)
+                nc.sync.dma_start(
+                    out=out_0[ms[ml], f * HEADS_PER_TILE:(f + 1) * HEADS_PER_TILE, :, :].rearrange("h s d -> s h d"),
+                    in_=hold["a"][:, ml, :].rearrange("p (h d) -> p h d", d=HD),
+                )
+
             fills.append((440, lambda: mul_sin(0)))
             fills.append((440, lambda: mul_sin(1)))
+            fills.append((440, lambda: mul_cos(0)))
+            fills.append((440, lambda: mul_cos(1)))
+            fills.append((440, lambda: add_store(0)))
+            fills.append((440, lambda: add_store(1)))
 
         def read_v(i, ms):
             f = FT_ORDER[i][1]
@@ -293,8 +297,6 @@ def tile_attention_pb_kernel(tc, key_value, wk, bk, wv, bv, cos, sin, out_0, out
         t_run_x(1)
         bias_mm(2, "s")
         bias_mm(3, "v")
-        nc.tensor.matmul(out=tab[:, 0, :], lhsT=identb[:], rhs=cosb[:], start=True, stop=True)
-        nc.tensor.matmul(out=tab[:, 1, :], lhsT=identb[:], rhs=nsin[:], start=True, stop=True)
         quant_x(1)
         load_ft(4)
         t_run_w(0)

@@ -22,7 +22,6 @@ FT_ORDER = (("k", 0), ("k", 1), ("v", 0), ("k", 2), ("k", 3), ("v", 1), ("v", 2)
 KHALF_FTS = 2
 RAW_BUFS = 20
 N_WARM = 6
-FILL_NS = 1600
 REORD_RBS = (0, 1)
 FIRST_REORD_RUN = 3
 
@@ -37,11 +36,12 @@ def tile_attention_pb_kernel(tc, key_value, wk, bk, wv, bv, cos, sin, out_0, out
         rawp = ctx.enter_context(tc.tile_pool(name="rawp", bufs=RAW_BUFS))
         rop = ctx.enter_context(tc.tile_pool(name="rop", bufs=6))
         grp = ctx.enter_context(tc.tile_pool(name="grp", bufs=3))
-        codep = ctx.enter_context(tc.tile_pool(name="codep", bufs=6))
+        codep = ctx.enter_context(tc.tile_pool(name="codep", bufs=5))
         kep = ctx.enter_context(tc.tile_pool(name="kep", bufs=3))
         vep = ctx.enter_context(tc.tile_pool(name="vep", bufs=6))
         tps = ctx.enter_context(tc.psum_pool(name="tps", bufs=4))
-        accp = ctx.enter_context(tc.psum_pool(name="accp", bufs=4))
+        accp = ctx.enter_context(tc.psum_pool(name="accp", bufs=3))
+        tabp = ctx.enter_context(tc.psum_pool(name="tabp", bufs=1))
         ctx.enter_context(tc.manual_schedule())
 
         warm = const.tile([P, N_TILE], BF16, name="warm")
@@ -214,67 +214,61 @@ def tile_attention_pb_kernel(tc, key_value, wk, bk, wv, bv, cos, sin, out_0, out
                 )
             accs[(i, m)] = acc
 
-        fills = []
-        fill_state = {"next": 0, "credit": 0}
-
-        def emit_fills(budget):
-            fill_state["credit"] = min(fill_state["credit"] + budget, 2 * budget)
-            while fill_state["next"] < len(fills):
-                cost, fn = fills[fill_state["next"]]
-                if cost > fill_state["credit"]:
-                    break
-                fn()
-                fill_state["credit"] -= cost
-                fill_state["next"] += 1
-
         def heads(ap):
             return ap.rearrange("p m (h d) -> p (m h) d", d=HD)
 
+        def bank_heads(ap):
+            return ap.rearrange("p (h d) -> p h d", d=HD)
+
+        tab = tabp.tile([P, 2, HD], F32, name="tab")
+        jobs = []
+        job_state = {"next": 0, "cur": None}
+
         def read_k(i, ms):
-            f = FT_ORDER[i][1]
-            t = kep.tile([P, 2, N_TILE], F32, name="t", tag="t", bufs=4)
+            t = kep.tile([P, 2, N_TILE], F32, name="t", tag="t")
             for ml in range(2):
                 nc.vector.tensor_tensor(out=t[:, ml, :], in0=accs[(i, ms[ml])][:], in1=bias[i][:], op=ADD)
-            hold = {}
+            jobs.append({"t": t, "ms": ms, "f": FT_ORDER[i][1]})
+
+        def pre_job():
+            if job_state["next"] == len(jobs):
+                return
+            job = jobs[job_state["next"]]
+            job_state["next"] += 1
+            job_state["cur"] = job
+            a = kep.tile([P, 2, N_TILE], F32, name="a", tag="a", bufs=6)
+            b = kep.tile([P, 2, N_TILE], F32, name="b", tag="b", bufs=2)
+            job["a"] = a
+            job["b"] = b
             nh = 2 * HEADS_PER_TILE
+            nc.vector.tensor_tensor(
+                out=heads(a[:]), in0=heads(job["t"][:]), in1=tab[:, 0, :].unsqueeze(1).to_broadcast([P, nh, HD]), op=MULT
+            )
+            nc.vector.tensor_tensor(
+                out=heads(b[:])[:, :, 0:64],
+                in0=heads(job["t"][:])[:, :, 64:128],
+                in1=tab[:, 1, 0:64].unsqueeze(1).to_broadcast([P, nh, 64]),
+                op=MULT,
+            )
 
-            def mul_sin(half):
-                if half == 0:
-                    b = kep.tile([P, 2, N_TILE], F32, name="b", tag="b")
-                    hold["b"] = b
-                dst = slice(64 * half, 64 * half + 64)
-                src = slice(64 - 64 * half, 128 - 64 * half)
+        def post_job():
+            job = job_state["cur"]
+            if job is None:
+                return
+            job_state["cur"] = None
+            f = job["f"]
+            for ml in range(2):
                 nc.vector.tensor_tensor(
-                    out=heads(hold["b"][:])[:, :, dst],
-                    in0=heads(t[:])[:, :, src],
-                    in1=nsin[:, dst].unsqueeze(1).to_broadcast([P, nh, 64]),
+                    out=bank_heads(job["b"][:, ml, :])[:, :, 64:128],
+                    in0=bank_heads(job["t"][:, ml, :])[:, :, 0:64],
+                    in1=tab[:, 1, 64:128].unsqueeze(1).to_broadcast([P, HEADS_PER_TILE, 64]),
                     op=MULT,
                 )
-
-            def mul_cos(ml):
-                if ml == 0:
-                    a = kep.tile([P, 2, N_TILE], F32, name="a", tag="a")
-                    hold["a"] = a
-                nc.vector.tensor_tensor(
-                    out=hold["a"][:, ml, :].rearrange("p (h d) -> p h d", d=HD),
-                    in0=t[:, ml, :].rearrange("p (h d) -> p h d", d=HD),
-                    in1=cosb[:].unsqueeze(1).to_broadcast([P, HEADS_PER_TILE, HD]),
-                    op=MULT,
-                )
-
-            def add_store(ml):
-                nc.vector.tensor_tensor(out=hold["a"][:, ml, :], in0=hold["a"][:, ml, :], in1=hold["b"][:, ml, :], op=ADD)
+                nc.gpsimd.tensor_tensor(out=job["a"][:, ml, :], in0=job["a"][:, ml, :], in1=job["b"][:, ml, :], op=ADD)
                 nc.sync.dma_start(
-                    out=out_0[ms[ml], f * HEADS_PER_TILE:(f + 1) * HEADS_PER_TILE, :, :].rearrange("h s d -> s h d"),
-                    in_=hold["a"][:, ml, :].rearrange("p (h d) -> p h d", d=HD),
+                    out=out_0[job["ms"][ml], f * HEADS_PER_TILE:(f + 1) * HEADS_PER_TILE, :, :].rearrange("h s d -> s h d"),
+                    in_=bank_heads(job["a"][:, ml, :]),
                 )
-
-            fills.append((440, lambda: mul_sin(0)))
-            fills.append((440, lambda: mul_sin(1)))
-            fills.append((440, lambda: mul_cos(0)))
-            fills.append((440, lambda: mul_cos(1)))
-            fills.append((440, lambda: add_store(0)))
-            fills.append((440, lambda: add_store(1)))
 
         def read_v(i, ms):
             f = FT_ORDER[i][1]
@@ -297,6 +291,8 @@ def tile_attention_pb_kernel(tc, key_value, wk, bk, wv, bv, cos, sin, out_0, out
         t_run_x(1)
         bias_mm(2, "s")
         bias_mm(3, "v")
+        nc.tensor.matmul(out=tab[:, 0, :], lhsT=identb[:], rhs=cosb[:], start=True, stop=True)
+        nc.tensor.matmul(out=tab[:, 1, :], lhsT=identb[:], rhs=nsin[:], start=True, stop=True)
         quant_x(1)
         load_ft(4)
         t_run_w(0)
@@ -318,9 +314,10 @@ def tile_attention_pb_kernel(tc, key_value, wk, bk, wv, bv, cos, sin, out_0, out
                 load_ft(6)
             if p == 3:
                 load_ft(7)
-            emit_fills(FILL_NS if p < n_runs - 3 else 1000000)
+            pre_job()
             if p + 2 < n_runs:
                 quant_w(p + 2)
+            post_job()
             i = p // 2
             ms = (2 * (p % 2), 2 * (p % 2) + 1)
             for m in ms:
@@ -329,4 +326,4 @@ def tile_attention_pb_kernel(tc, key_value, wk, bk, wv, bv, cos, sin, out_0, out
                 read_k(i, ms)
             else:
                 read_v(i, ms)
-        emit_fills(1000000)
+        assert job_state["next"] == len(jobs) and job_state["cur"] is None

@@ -24,6 +24,7 @@ RAW_BUFS = 20
 N_WARM = 6
 REORD_RBS = (0, 1)
 FIRST_REORD_RUN = 3
+REORD_AHEAD = 4
 
 
 def tile_attention_pb_kernel(tc, key_value, wk, bk, wv, bv, cos, sin, out_0, out_1):
@@ -305,11 +306,13 @@ def tile_attention_pb_kernel(tc, key_value, wk, bk, wv, bv, cos, sin, out_0, out
         quant_w(1)
         load_ft(5)
 
+        reord_state = {"next": FIRST_REORD_RUN}
         for p in range(n_runs):
             if p + 2 < n_runs:
                 t_run_w(p + 2)
-            if FIRST_REORD_RUN <= p + 3 < n_runs:
-                reorder_run(p + 3)
+            while reord_state["next"] < min(n_runs, p + (4 if p == 0 else REORD_AHEAD + 1)):
+                reorder_run(reord_state["next"])
+                reord_state["next"] += 1
             if p == 1:
                 load_ft(6)
             if p == 3:

@@ -25,6 +25,7 @@ N_WARM = 6
 REORD_RBS = (0, 1)
 FIRST_REORD_RUN = 3
 REORD_AHEAD = 4
+N_BIAS_MM = 2
 
 
 def tile_attention_pb_kernel(tc, key_value, wk, bk, wv, bv, cos, sin, out_0, out_1):
@@ -59,7 +60,6 @@ def tile_attention_pb_kernel(tc, key_value, wk, bk, wv, bv, cos, sin, out_0, out
         nc.scalar.dma_start(out=sinb[:], in_=sin.flatten_outer_dims())
         nc.scalar.dma_start(out=cosb[:], in_=cos.flatten_outer_dims())
         nc.scalar.dma_start(out=brows[0:4, :], in_=bk.rearrange("(f n) -> f n", n=N_TILE))
-        nc.scalar.dma_start(out=brows[4:8, :], in_=bv.rearrange("(f n) -> f n", n=N_TILE))
         scratch = const.tile([P, 1], F32, name="scratch")
         nc.scalar.copy(out=scratch[:], in_=warm[:, 0:1])
 
@@ -106,6 +106,11 @@ def tile_attention_pb_kernel(tc, key_value, wk, bk, wv, bv, cos, sin, out_0, out
         for i in range(4):
             load_ft(i)
 
+        bk_late = const.tile([P, E - N_BIAS_MM * N_TILE], BF16, name="bk_late")
+        nc.sync.dma_start(out=bk_late[:], in_=bk[N_BIAS_MM * N_TILE:E].partition_broadcast(P))
+        bv_all = const.tile([P, E], BF16, name="bv_all")
+        nc.sync.dma_start(out=bv_all[:], in_=bv.partition_broadcast(P))
+
         nsin = const.tile([P, HD], BF16, name="nsin")
         nc.vector.tensor_scalar(out=nsin[:, 0:64], in0=sinb[:, 0:64], scalar1=-1.0, scalar2=None, op0=MULT)
         nc.vector.tensor_copy(out=nsin[:, 64:128], in_=sinb[:, 64:128])
@@ -128,7 +133,7 @@ def tile_attention_pb_kernel(tc, key_value, wk, bk, wv, bv, cos, sin, out_0, out
                 nc.scalar.copy(out=bt[:], in_=ps[:])
             else:
                 nc.vector.tensor_copy(out=bt[:], in_=ps[:])
-            bias[i] = bt
+            bias[i] = bt[:]
 
         xg = {}
         xcodes = {}
@@ -228,7 +233,7 @@ def tile_attention_pb_kernel(tc, key_value, wk, bk, wv, bv, cos, sin, out_0, out
         def read_k(i, ms):
             t = kep.tile([P, 2, N_TILE], F32, name="t", tag="t")
             for ml in range(2):
-                nc.vector.tensor_tensor(out=t[:, ml, :], in0=accs[(i, ms[ml])][:], in1=bias[i][:], op=ADD)
+                nc.vector.tensor_tensor(out=t[:, ml, :], in0=accs[(i, ms[ml])][:], in1=bias[i], op=ADD)
             jobs.append({"t": t, "ms": ms, "f": FT_ORDER[i][1]})
 
         def pre_job():
@@ -275,11 +280,18 @@ def tile_attention_pb_kernel(tc, key_value, wk, bk, wv, bv, cos, sin, out_0, out
             f = FT_ORDER[i][1]
             for m in ms:
                 vout = vep.tile([P, N_TILE], F32, name="vout", tag="vout")
-                nc.vector.tensor_tensor(out=vout[:], in0=accs[(i, m)][:], in1=bias[i][:], op=ADD)
+                nc.vector.tensor_tensor(out=vout[:], in0=accs[(i, m)][:], in1=bias[i], op=ADD)
                 nc.sync.dma_start(
                     out=out_1[m, f * HEADS_PER_TILE:(f + 1) * HEADS_PER_TILE, :, :].rearrange("h s d -> s h d"),
                     in_=vout[:].rearrange("p (h d) -> p h d", d=HD),
                 )
+
+        for i in range(N_BIAS_MM, len(FT_ORDER)):
+            which, f = FT_ORDER[i]
+            if which == "k":
+                bias[i] = bk_late[:, (f - N_BIAS_MM) * N_TILE:(f - N_BIAS_MM + 1) * N_TILE]
+            else:
+                bias[i] = bv_all[:, f * N_TILE:(f + 1) * N_TILE]
 
         wps = accp.tile([P, N_TILE], F32, name="acc", tag="acc")
         for n in range(N_WARM):
@@ -290,19 +302,13 @@ def tile_attention_pb_kernel(tc, key_value, wk, bk, wv, bv, cos, sin, out_0, out
         bias_mm(1, "v")
         quant_x(0)
         t_run_x(1)
-        bias_mm(2, "s")
-        bias_mm(3, "v")
         nc.tensor.matmul(out=tab[:, 0, :], lhsT=identb[:], rhs=cosb[:], start=True, stop=True)
         nc.tensor.matmul(out=tab[:, 1, :], lhsT=identb[:], rhs=nsin[:], start=True, stop=True)
         quant_x(1)
         load_ft(4)
         t_run_w(0)
-        bias_mm(4, "s")
-        bias_mm(5, "v")
         quant_w(0)
         t_run_w(1)
-        bias_mm(6, "s")
-        bias_mm(7, "v")
         quant_w(1)
         load_ft(5)
 

@@ -23,8 +23,9 @@ KHALF_FTS = 2
 RAW_BUFS = 20
 N_WARM = 6
 REORD_RBS = (0, 1)
-FIRST_REORD_RUN = 3
+FIRST_REORD_RUN = 4
 REORD_AHEAD = 4
+TWO_JOB_PERIODS = (4, 8, 11)
 N_BIAS_MM = 2
 
 
@@ -64,10 +65,14 @@ def tile_attention_pb_kernel(tc, key_value, wk, bk, wv, bv, cos, sin, out_0, out
         nc.scalar.copy(out=scratch[:], in_=warm[:, 0:1])
 
         xraw = []
-        for m in range(B):
+
+        def load_x(m):
             xt = rawp.tile([P, DIM], BF16, name="raw", tag="raw")
             nc.sync.dma_start(out=xt[:], in_=xf[m * P:(m + 1) * P, :])
             xraw.append(xt)
+
+        load_x(0)
+        load_x(1)
 
         wtiles = {}
 
@@ -103,7 +108,10 @@ def tile_attention_pb_kernel(tc, key_value, wk, bk, wv, bv, cos, sin, out_0, out
                 base = kh * 512
             return wt[:].bitcast(F32)[:, base:base + 512]
 
-        for i in range(4):
+        load_ft(0)
+        load_x(2)
+        load_x(3)
+        for i in range(1, 4):
             load_ft(i)
 
         bk_late = const.tile([P, E - N_BIAS_MM * N_TILE], BF16, name="bk_late")
@@ -220,21 +228,19 @@ def tile_attention_pb_kernel(tc, key_value, wk, bk, wv, bv, cos, sin, out_0, out
                 )
             accs[(i, m)] = acc
 
-        def heads(ap):
-            return ap.rearrange("p m (h d) -> p (m h) d", d=HD)
-
         def bank_heads(ap):
             return ap.rearrange("p (h d) -> p h d", d=HD)
 
         tab = tabp.tile([P, 2, HD], F32, name="tab")
         jobs = []
+        unsent = []
         job_state = {"next": 0, "cur": None}
 
         def read_k(i, ms):
-            t = kep.tile([P, 2, N_TILE], F32, name="t", tag="t")
-            for ml in range(2):
-                nc.vector.tensor_tensor(out=t[:, ml, :], in0=accs[(i, ms[ml])][:], in1=bias[i], op=ADD)
-            jobs.append({"t": t, "ms": ms, "f": FT_ORDER[i][1]})
+            for m in ms:
+                t = kep.tile([P, N_TILE], F32, name="t", tag="t", bufs=8)
+                nc.vector.tensor_tensor(out=t[:], in0=accs[(i, m)][:], in1=bias[i], op=ADD)
+                jobs.append({"t": t, "m": m, "f": FT_ORDER[i][1]})
 
         def pre_job():
             if job_state["next"] == len(jobs):
@@ -242,17 +248,17 @@ def tile_attention_pb_kernel(tc, key_value, wk, bk, wv, bv, cos, sin, out_0, out
             job = jobs[job_state["next"]]
             job_state["next"] += 1
             job_state["cur"] = job
-            a = kep.tile([P, 2, N_TILE], F32, name="a", tag="a", bufs=6)
-            b = kep.tile([P, 2, N_TILE], F32, name="b", tag="b", bufs=2)
+            a = kep.tile([P, N_TILE], F32, name="a", tag="a", bufs=12)
+            b = kep.tile([P, N_TILE], F32, name="b", tag="b", bufs=3)
             job["a"] = a
             job["b"] = b
-            nh = 2 * HEADS_PER_TILE
+            nh = HEADS_PER_TILE
             nc.vector.tensor_tensor(
-                out=heads(a[:]), in0=heads(job["t"][:]), in1=tab[:, 0, :].unsqueeze(1).to_broadcast([P, nh, HD]), op=MULT
+                out=bank_heads(a[:]), in0=bank_heads(job["t"][:]), in1=tab[:, 0, :].unsqueeze(1).to_broadcast([P, nh, HD]), op=MULT
             )
             nc.vector.tensor_tensor(
-                out=heads(b[:])[:, :, 0:64],
-                in0=heads(job["t"][:])[:, :, 64:128],
+                out=bank_heads(b[:])[:, :, 0:64],
+                in0=bank_heads(job["t"][:])[:, :, 64:128],
                 in1=tab[:, 1, 0:64].unsqueeze(1).to_broadcast([P, nh, 64]),
                 op=MULT,
             )
@@ -263,18 +269,23 @@ def tile_attention_pb_kernel(tc, key_value, wk, bk, wv, bv, cos, sin, out_0, out
                 return
             job_state["cur"] = None
             f = job["f"]
-            for ml in range(2):
-                nc.vector.tensor_tensor(
-                    out=bank_heads(job["b"][:, ml, :])[:, :, 64:128],
-                    in0=bank_heads(job["t"][:, ml, :])[:, :, 0:64],
-                    in1=tab[:, 1, 64:128].unsqueeze(1).to_broadcast([P, HEADS_PER_TILE, 64]),
-                    op=MULT,
-                )
-                nc.gpsimd.tensor_tensor(out=job["a"][:, ml, :], in0=job["a"][:, ml, :], in1=job["b"][:, ml, :], op=ADD)
+            nc.vector.tensor_tensor(
+                out=bank_heads(job["b"][:])[:, :, 64:128],
+                in0=bank_heads(job["t"][:])[:, :, 0:64],
+                in1=tab[:, 1, 64:128].unsqueeze(1).to_broadcast([P, HEADS_PER_TILE, 64]),
+                op=MULT,
+            )
+            nc.gpsimd.tensor_tensor(out=job["a"][:], in0=job["a"][:], in1=job["b"][:], op=ADD)
+            unsent.append(job)
+
+        def send_k():
+            for job in unsent:
+                f = job["f"]
                 nc.sync.dma_start(
-                    out=out_0[job["ms"][ml], f * HEADS_PER_TILE:(f + 1) * HEADS_PER_TILE, :, :].rearrange("h s d -> s h d"),
-                    in_=bank_heads(job["a"][:, ml, :]),
+                    out=out_0[job["m"], f * HEADS_PER_TILE:(f + 1) * HEADS_PER_TILE, :, :].rearrange("h s d -> s h d"),
+                    in_=bank_heads(job["a"][:]),
                 )
+            unsent.clear()
 
         def read_v(i, ms):
             f = FT_ORDER[i][1]
@@ -301,32 +312,20 @@ def tile_attention_pb_kernel(tc, key_value, wk, bk, wv, bv, cos, sin, out_0, out
         bias_mm(0, "s")
         bias_mm(1, "v")
         quant_x(0)
-        t_run_x(1)
-        nc.tensor.matmul(out=tab[:, 0, :], lhsT=identb[:], rhs=cosb[:], start=True, stop=True)
-        nc.tensor.matmul(out=tab[:, 1, :], lhsT=identb[:], rhs=nsin[:], start=True, stop=True)
-        quant_x(1)
-        load_ft(4)
         t_run_w(0)
         quant_w(0)
         t_run_w(1)
+        nc.tensor.matmul(out=tab[:, 0, :], lhsT=identb[:], rhs=cosb[:], start=True, stop=True)
+        nc.tensor.matmul(out=tab[:, 1, :], lhsT=identb[:], rhs=nsin[:], start=True, stop=True)
         quant_w(1)
+        t_run_x(1)
+        quant_x(1)
+        load_ft(4)
         load_ft(5)
 
         reord_state = {"next": FIRST_REORD_RUN}
-        for p in range(n_runs):
-            if p + 2 < n_runs:
-                t_run_w(p + 2)
-            while reord_state["next"] < min(n_runs, p + (4 if p == 0 else REORD_AHEAD + 1)):
-                reorder_run(reord_state["next"])
-                reord_state["next"] += 1
-            if p == 1:
-                load_ft(6)
-            if p == 3:
-                load_ft(7)
-            pre_job()
-            if p + 2 < n_runs:
-                quant_w(p + 2)
-            post_job()
+
+        def products(p):
             i = p // 2
             ms = (2 * (p % 2), 2 * (p % 2) + 1)
             for m in ms:
@@ -335,4 +334,27 @@ def tile_attention_pb_kernel(tc, key_value, wk, bk, wv, bv, cos, sin, out_0, out
                 read_k(i, ms)
             else:
                 read_v(i, ms)
-        assert job_state["next"] == len(jobs) and job_state["cur"] is None
+
+        for p in range(n_runs):
+            if p == 0:
+                products(p)
+            if p + 2 < n_runs:
+                t_run_w(p + 2)
+            while reord_state["next"] < min(n_runs, p + (REORD_AHEAD if p == 0 else REORD_AHEAD + 1)):
+                reorder_run(reord_state["next"])
+                reord_state["next"] += 1
+            if p == 1:
+                load_ft(6)
+            if p == 3:
+                load_ft(7)
+            send_k()
+            pre_job()
+            if p + 2 < n_runs:
+                quant_w(p + 2)
+            post_job()
+            if p in TWO_JOB_PERIODS:
+                pre_job()
+                post_job()
+            if p > 0:
+                products(p)
+        assert job_state["next"] == len(jobs) and job_state["cur"] is None and not unsent

@@ -309,8 +309,6 @@ def tile_attention_pb_kernel(tc, key_value, wk, bk, wv, bv, cos, sin, out_0, out
             nc.tensor.matmul(out=wps[:], lhsT=warm[:, 0:P], rhs=warm[:], start=True, stop=True)
 
         t_run_x(0)
-        bias_mm(0, "s")
-        bias_mm(1, "v")
         quant_x(0)
         t_run_w(0)
         quant_w(0)
@@ -318,6 +316,8 @@ def tile_attention_pb_kernel(tc, key_value, wk, bk, wv, bv, cos, sin, out_0, out
         nc.tensor.matmul(out=tab[:, 0, :], lhsT=identb[:], rhs=cosb[:], start=True, stop=True)
         nc.tensor.matmul(out=tab[:, 1, :], lhsT=identb[:], rhs=nsin[:], start=True, stop=True)
         quant_w(1)
+        bias_mm(0, "s")
+        bias_mm(1, "v")
         t_run_x(1)
         quant_x(1)
         load_ft(4)
@@ -337,7 +337,8 @@ def tile_attention_pb_kernel(tc, key_value, wk, bk, wv, bv, cos, sin, out_0, out
 
         for p in range(n_runs):
             if p == 0:
-                products(p)
+                m_group(0, 0)
+                read_k(0, (0,))
             if p + 2 < n_runs:
                 t_run_w(p + 2)
             while reord_state["next"] < min(n_runs, p + (REORD_AHEAD if p == 0 else REORD_AHEAD + 1)):
@@ -355,6 +356,9 @@ def tile_attention_pb_kernel(tc, key_value, wk, bk, wv, bv, cos, sin, out_0, out
             if p in TWO_JOB_PERIODS:
                 pre_job()
                 post_job()
-            if p > 0:
+            if p == 0:
+                m_group(0, 1)
+                read_k(0, (1,))
+            else:
                 products(p)
         assert job_state["next"] == len(jobs) and job_state["cur"] is None and not unsent

@@ -19,7 +19,7 @@ P = 128
 N_TILE = 512
 HEADS_PER_TILE = N_TILE // HD
 FT_ORDER = (("k", 0), ("k", 1), ("v", 0), ("k", 2), ("k", 3), ("v", 1), ("v", 2), ("v", 3))
-KHALF_FTS = 2
+KHALF_FTS = 3
 RAW_BUFS = 20
 N_WARM = 6
 REORD_RBS = (0, 1)
@@ -291,11 +291,20 @@ def tile_attention_pb_kernel(tc, key_value, wk, bk, wv, bv, cos, sin, out_0, out
             f = FT_ORDER[i][1]
             for m in ms:
                 vout = vep.tile([P, N_TILE], F32, name="vout", tag="vout")
-                nc.vector.tensor_tensor(out=vout[:], in0=accs[(i, m)][:], in1=bias[i], op=ADD)
-                nc.sync.dma_start(
-                    out=out_1[m, f * HEADS_PER_TILE:(f + 1) * HEADS_PER_TILE, :, :].rearrange("h s d -> s h d"),
-                    in_=vout[:].rearrange("p (h d) -> p h d", d=HD),
-                )
+                pieces = 1
+                if i == len(FT_ORDER) - 1 and m == B - 1:
+                    pieces = 4
+                if i == len(FT_ORDER) - 1 and m == B - 2:
+                    pieces = 2
+                hp = HEADS_PER_TILE // pieces
+                for q in range(pieces):
+                    cols = slice(q * hp * HD, (q + 1) * hp * HD)
+                    nc.vector.tensor_tensor(out=vout[:, cols], in0=accs[(i, m)][:, cols], in1=bias[i][:, cols], op=ADD)
+                    h0 = f * HEADS_PER_TILE + q * hp
+                    nc.sync.dma_start(
+                        out=out_1[m, h0:h0 + hp, :, :].rearrange("h s d -> s h d"),
+                        in_=vout[:, cols].rearrange("p (h d) -> p h d", d=HD),
+                    )
 
         for i in range(N_BIAS_MM, len(FT_ORDER)):
             which, f = FT_ORDER[i]

@@ -22,7 +22,7 @@ FT_ORDER = (("k", 0), ("k", 1), ("v", 0), ("k", 2), ("k", 3), ("v", 1), ("v", 2)
 KHALF_FTS = 3
 RAW_BUFS = 20
 N_WARM = 6
-REORD_RBS = (0, 1)
+REORD_RBS = (0, 1, 2)
 FIRST_REORD_RUN = 4
 REORD_AHEAD = 4
 TWO_JOB_PERIODS = (4, 8, 11)
@@ -37,7 +37,7 @@ def tile_attention_pb_kernel(tc, key_value, wk, bk, wv, bv, cos, sin, out_0, out
     with ExitStack() as ctx:
         const = ctx.enter_context(tc.tile_pool(name="const", bufs=1))
         rawp = ctx.enter_context(tc.tile_pool(name="rawp", bufs=RAW_BUFS))
-        rop = ctx.enter_context(tc.tile_pool(name="rop", bufs=6))
+        rop = ctx.enter_context(tc.tile_pool(name="rop", bufs=9))
         grp = ctx.enter_context(tc.tile_pool(name="grp", bufs=3))
         codep = ctx.enter_context(tc.tile_pool(name="codep", bufs=5))
         kep = ctx.enter_context(tc.tile_pool(name="kep", bufs=3))

@@ -231,7 +231,8 @@ def tile_attention_pb_kernel(tc, key_value, wk, bk, wv, bv, cos, sin, out_0, out
         def bank_heads(ap):
             return ap.rearrange("p (h d) -> p h d", d=HD)
 
-        tab = tabp.tile([P, 2, HD], F32, name="tab")
+        tab = tabp.tile([P, 2, 2, 64], F32, name="tab")
+        gdep = const.tile([P, 1], U32, name="gdep")
         jobs = []
         unsent = []
         job_state = {"next": 0, "cur": None}
@@ -248,34 +249,27 @@ def tile_attention_pb_kernel(tc, key_value, wk, bk, wv, bv, cos, sin, out_0, out
             job = jobs[job_state["next"]]
             job_state["next"] += 1
             job_state["cur"] = job
-            a = kep.tile([P, N_TILE], F32, name="a", tag="a", bufs=12)
-            b = kep.tile([P, N_TILE], F32, name="b", tag="b", bufs=3)
-            job["a"] = a
-            job["b"] = b
+            ab = kep.tile([P, 2 * N_TILE], F32, name="ab", tag="ab", bufs=3)
+            job["ab"] = ab
             nh = HEADS_PER_TILE
             nc.vector.tensor_tensor(
-                out=bank_heads(a[:]), in0=bank_heads(job["t"][:]), in1=tab[:, 0, :].unsqueeze(1).to_broadcast([P, nh, HD]), op=MULT
-            )
-            nc.vector.tensor_tensor(
-                out=bank_heads(b[:])[:, :, 0:64],
-                in0=bank_heads(job["t"][:])[:, :, 64:128],
-                in1=tab[:, 1, 0:64].unsqueeze(1).to_broadcast([P, nh, 64]),
+                out=ab[:].rearrange("p (h s y d) -> p h s y d", s=2, y=2, d=64),
+                in0=job["t"][:].rearrange("p (h s d) -> p h s d", s=2, d=64).unsqueeze(3).to_broadcast([P, nh, 2, 2, 64]),
+                in1=tab[:].unsqueeze(1).to_broadcast([P, nh, 2, 2, 64]),
                 op=MULT,
             )
 
-        def post_job():
+        def post_job(after_quant):
             job = job_state["cur"]
             if job is None:
                 return
             job_state["cur"] = None
-            f = job["f"]
-            nc.vector.tensor_tensor(
-                out=bank_heads(job["b"][:])[:, :, 64:128],
-                in0=bank_heads(job["t"][:])[:, :, 0:64],
-                in1=tab[:, 1, 64:128].unsqueeze(1).to_broadcast([P, HEADS_PER_TILE, 64]),
-                op=MULT,
-            )
-            nc.gpsimd.tensor_tensor(out=job["a"][:], in0=job["a"][:], in1=job["b"][:], op=ADD)
+            if after_quant is not None:
+                nc.gpsimd.tensor_copy(out=gdep[:], in_=wcodes[after_quant][:, 0:1])
+            a = kep.tile([P, N_TILE], F32, name="a", tag="a", bufs=12)
+            job["a"] = a
+            abv = job["ab"][:].rearrange("p (h s e) -> p h s e", s=2, e=HD)
+            nc.gpsimd.tensor_tensor(out=bank_heads(a[:]), in0=abv[:, :, 0, :], in1=abv[:, :, 1, :], op=ADD)
             unsent.append(job)
 
         def send_k():
@@ -322,8 +316,10 @@ def tile_attention_pb_kernel(tc, key_value, wk, bk, wv, bv, cos, sin, out_0, out
         t_run_w(0)
         quant_w(0)
         t_run_w(1)
-        nc.tensor.matmul(out=tab[:, 0, :], lhsT=identb[:], rhs=cosb[:], start=True, stop=True)
-        nc.tensor.matmul(out=tab[:, 1, :], lhsT=identb[:], rhs=nsin[:], start=True, stop=True)
+        nc.tensor.matmul(out=tab[:, 0, 0, :], lhsT=identb[:], rhs=cosb[:, 0:64], start=True, stop=True)
+        nc.tensor.matmul(out=tab[:, 0, 1, :], lhsT=identb[:], rhs=nsin[:, 64:128], start=True, stop=True)
+        nc.tensor.matmul(out=tab[:, 1, 0, :], lhsT=identb[:], rhs=nsin[:, 0:64], start=True, stop=True)
+        nc.tensor.matmul(out=tab[:, 1, 1, :], lhsT=identb[:], rhs=cosb[:, 64:128], start=True, stop=True)
         quant_w(1)
         bias_mm(0, "s")
         bias_mm(1, "v")
@@ -361,10 +357,10 @@ def tile_attention_pb_kernel(tc, key_value, wk, bk, wv, bv, cos, sin, out_0, out
             pre_job()
             if p + 2 < n_runs:
                 quant_w(p + 2)
-            post_job()
+            post_job(p + 2 if p + 2 < n_runs else None)
             if p in TWO_JOB_PERIODS:
                 pre_job()
-                post_job()
+                post_job(None)
             if p == 0:
                 m_group(0, 1)
                 read_k(0, (1,))

@@ -21,7 +21,7 @@ HEADS_PER_TILE = N_TILE // HD
 FT_ORDER = (("k", 0), ("k", 1), ("v", 0), ("k", 2), ("k", 3), ("v", 1), ("v", 2), ("v", 3))
 KHALF_FTS = 3
 RAW_BUFS = 20
-N_WARM = 6
+N_WARM = 2
 REORD_RBS = (0, 1, 2)
 FIRST_REORD_RUN = 4
 REORD_AHEAD = 4
@@ -68,7 +68,10 @@ def tile_attention_pb_kernel(tc, key_value, wk, bk, wv, bv, cos, sin, out_0, out
 
         def load_x(m):
             xt = rawp.tile([P, DIM], BF16, name="raw", tag="raw")
-            nc.sync.dma_start(out=xt[:], in_=xf[m * P:(m + 1) * P, :])
+            pieces = 2 if m == 0 else 1
+            w = DIM // pieces
+            for q in range(pieces):
+                nc.sync.dma_start(out=xt[:, q * w:(q + 1) * w], in_=xf[m * P:(m + 1) * P, q * w:(q + 1) * w])
             xraw.append(xt)
 
         load_x(0)
@@ -119,9 +122,11 @@ def tile_attention_pb_kernel(tc, key_value, wk, bk, wv, bv, cos, sin, out_0, out
         bv_all = const.tile([P, E], BF16, name="bv_all")
         nc.sync.dma_start(out=bv_all[:], in_=bv.partition_broadcast(P))
 
-        nsin = const.tile([P, HD], BF16, name="nsin")
-        nc.vector.tensor_scalar(out=nsin[:, 0:64], in0=sinb[:, 0:64], scalar1=-1.0, scalar2=None, op0=MULT)
-        nc.vector.tensor_copy(out=nsin[:, 64:128], in_=sinb[:, 64:128])
+        tabsrc = const.tile([P, 2 * HD], BF16, name="tabsrc")
+        nc.vector.tensor_copy(out=tabsrc[:, 0:64], in_=cosb[:, 0:64])
+        nc.vector.tensor_copy(out=tabsrc[:, 64:128], in_=sinb[:, 64:128])
+        nc.vector.tensor_scalar(out=tabsrc[:, 128:192], in0=sinb[:, 0:64], scalar1=-1.0, scalar2=None, op0=MULT)
+        nc.vector.tensor_copy(out=tabsrc[:, 192:256], in_=cosb[:, 64:128])
 
         def word_rows(g, lo, hi):
             return g[:].bitcast(F32).rearrange("p (r u) -> p r u", u=2)[:, lo:hi, :]
@@ -316,10 +321,7 @@ def tile_attention_pb_kernel(tc, key_value, wk, bk, wv, bv, cos, sin, out_0, out
         t_run_w(0)
         quant_w(0)
         t_run_w(1)
-        nc.tensor.matmul(out=tab[:, 0, 0, :], lhsT=identb[:], rhs=cosb[:, 0:64], start=True, stop=True)
-        nc.tensor.matmul(out=tab[:, 0, 1, :], lhsT=identb[:], rhs=nsin[:, 64:128], start=True, stop=True)
-        nc.tensor.matmul(out=tab[:, 1, 0, :], lhsT=identb[:], rhs=nsin[:, 0:64], start=True, stop=True)
-        nc.tensor.matmul(out=tab[:, 1, 1, :], lhsT=identb[:], rhs=cosb[:, 64:128], start=True, stop=True)
+        nc.tensor.matmul(out=tab[:].rearrange("p s y d -> p (s y d)"), lhsT=identb[:], rhs=tabsrc[:], start=True, stop=True)
         quant_w(1)
         bias_mm(0, "s")
         bias_mm(1, "v")

@@ -42,8 +42,7 @@ def tile_attention_pb_kernel(tc, key_value, wk, bk, wv, bv, cos, sin, out_0, out
         codep = ctx.enter_context(tc.tile_pool(name="codep", bufs=5))
         kep = ctx.enter_context(tc.tile_pool(name="kep", bufs=3))
         vep = ctx.enter_context(tc.tile_pool(name="vep", bufs=6))
-        tps = ctx.enter_context(tc.psum_pool(name="tps", bufs=4))
-        accp = ctx.enter_context(tc.psum_pool(name="accp", bufs=3))
+        bankp = ctx.enter_context(tc.psum_pool(name="bankp", bufs=7))
         tabp = ctx.enter_context(tc.psum_pool(name="tabp", bufs=1))
         ctx.enter_context(tc.manual_schedule())
 
@@ -139,7 +138,7 @@ def tile_attention_pb_kernel(tc, key_value, wk, bk, wv, bv, cos, sin, out_0, out
         def bias_mm(i, engine):
             which, f = FT_ORDER[i]
             row = f if which == "k" else 4 + f
-            ps = accp.tile([P, N_TILE], F32, name="acc", tag="acc")
+            ps = bankp.tile([P, N_TILE], F32, name="bank", tag="bank")
             nc.tensor.matmul(out=ps[:], lhsT=identb[:, row:row + 1].to_broadcast([P, P]), rhs=brows[:], start=True, stop=True)
             bt = const.tile([P, N_TILE], BF16, name="bias%d" % i)
             if engine == "s":
@@ -157,7 +156,7 @@ def tile_attention_pb_kernel(tc, key_value, wk, bk, wv, bv, cos, sin, out_0, out
             for ml in range(2):
                 words = xraw[2 * half + ml][:].bitcast(F32)
                 for ch in range(2):
-                    bank = tps.tile([P, 2, 256], F32, name="tp", tag="tp")
+                    bank = bankp.tile([P, 2, 256], F32, name="bank", tag="bank")
                     for cl in range(2):
                         c = 2 * ch + cl
                         for u in range(2):
@@ -194,7 +193,7 @@ def tile_attention_pb_kernel(tc, key_value, wk, bk, wv, bv, cos, sin, out_0, out
             g = grp.tile([P, 2 * DIM], BF16, name="grouped", tag="grouped", align_bytes=64)
             for pair in range(2):
                 for cl in range(2):
-                    bank = tps.tile([P, 2, 256], F32, name="tp", tag="tp")
+                    bank = bankp.tile([P, 2, 256], F32, name="bank", tag="bank")
                     for rl in range(2):
                         rb = 2 * pair + rl
                         for u in range(2):
@@ -217,7 +216,7 @@ def tile_attention_pb_kernel(tc, key_value, wk, bk, wv, bv, cos, sin, out_0, out
         accs = {}
 
         def m_group(i, m):
-            acc = accp.tile([P, N_TILE], F32, name="acc", tag="acc")
+            acc = bankp.tile([P, N_TILE], F32, name="bank", tag="bank")
             for c in range(4):
                 r = 2 * i + c // 2
                 wcol = slice((c % 2) * N_TILE, (c % 2 + 1) * N_TILE)
@@ -312,7 +311,7 @@ def tile_attention_pb_kernel(tc, key_value, wk, bk, wv, bv, cos, sin, out_0, out
             else:
                 bias[i] = bv_all[:, f * N_TILE:(f + 1) * N_TILE]
 
-        wps = accp.tile([P, N_TILE], F32, name="acc", tag="acc")
+        wps = bankp.tile([P, N_TILE], F32, name="bank", tag="bank")
         for n in range(N_WARM):
             nc.tensor.matmul(out=wps[:], lhsT=warm[:, 0:P], rhs=warm[:], start=True, stop=True)
 

@@ -180,14 +180,27 @@ def tile_attention_pb_kernel(tc, key_value, wk, bk, wv, bv, cos, sin, out_0, out
         wscales = {}
         reord = {}
 
+        v_reorders = []
+
         def reorder_run(r):
             for rb in REORD_RBS:
                 ro = rop.tile([P, 512], F32, name="ro", tag="ro")
+                reord[(r, rb)] = ro
+                if r == FIRST_REORD_RUN:
+                    v_reorders.append((r, rb))
+                    continue
                 nc.scalar.copy(
                     out=ro[:].rearrange("p (c u q) -> p c q u", c=2, u=2),
                     in_=run_words(r, rb).rearrange("p (c q u) -> p c q u", c=2, u=2),
                 )
-                reord[(r, rb)] = ro
+
+        def reorder_on_vector():
+            for r, rb in v_reorders:
+                nc.vector.tensor_copy(
+                    out=reord[(r, rb)][:].rearrange("p (c u q) -> p c q u", c=2, u=2),
+                    in_=run_words(r, rb).rearrange("p (c q u) -> p c q u", c=2, u=2),
+                )
+            v_reorders.clear()
 
         def t_run_w(r):
             g = grp.tile([P, 2 * DIM], BF16, name="grouped", tag="grouped", align_bytes=64)
@@ -356,6 +369,7 @@ def tile_attention_pb_kernel(tc, key_value, wk, bk, wv, bv, cos, sin, out_0, out
                 load_ft(7)
             send_k()
             pre_job()
+            reorder_on_vector()
             if p + 2 < n_runs:
                 quant_w(p + 2)
             post_job(p + 2 if p + 2 < n_runs else None)

from contextlib import ExitStack

import concourse.mybir as mybir
from concourse.masks import make_identity

B, S, DIM, H, HD = 4, 128, 2048, 16, 128
E = H * HD
FLOPS = 2 * 2 * B * S * DIM * E

F32 = mybir.dt.float32
BF16 = mybir.dt.bfloat16
U32 = mybir.dt.uint32
U8 = mybir.dt.uint8
FP8X4 = mybir.dt.float8_e5m2_x4
ADD = mybir.AluOpType.add
MULT = mybir.AluOpType.mult

P = 128
N_TILE = 512
HEADS_PER_TILE = N_TILE // HD
FT_ORDER = (("k", 0), ("k", 1), ("v", 0), ("k", 2), ("k", 3), ("v", 1), ("v", 2), ("v", 3))
KHALF_FTS = 3
RAW_BUFS = 20
N_WARM = 2
REORD_RBS = (0, 1, 2)
FIRST_REORD_RUN = 4
REORD_AHEAD = 4
TWO_JOB_PERIODS = (4, 8, 11)
N_BIAS_MM = 2


def tile_attention_pb_kernel(tc, key_value, wk, bk, wv, bv, cos, sin, out_0, out_1):
    nc = tc.nc
    xf = key_value.flatten_outer_dims()
    n_runs = 2 * len(FT_ORDER)

    with ExitStack() as ctx:
        const = ctx.enter_context(tc.tile_pool(name="const", bufs=1))
        rawp = ctx.enter_context(tc.tile_pool(name="rawp", bufs=RAW_BUFS))
        rop = ctx.enter_context(tc.tile_pool(name="rop", bufs=9))
        grp = ctx.enter_context(tc.tile_pool(name="grp", bufs=3))
        codep = ctx.enter_context(tc.tile_pool(name="codep", bufs=5))
        kep = ctx.enter_context(tc.tile_pool(name="kep", bufs=3))
        vep = ctx.enter_context(tc.tile_pool(name="vep", bufs=6))
        bankp = ctx.enter_context(tc.psum_pool(name="bankp", bufs=7))
        tabp = ctx.enter_context(tc.psum_pool(name="tabp", bufs=1))
        ctx.enter_context(tc.manual_schedule())

        warm = const.tile([P, N_TILE], BF16, name="warm")
        nc.vector.memset(warm[:], 0.0)
        brows = const.tile([P, N_TILE], BF16, name="brows")
        nc.vector.memset(brows[:], 0.0)
        ident = const.tile([P, P], F32, name="ident")
        make_identity(nc, ident[:])
        identb = const.tile([P, P], BF16, name="identb")
        make_identity(nc, identb[:])

        cosb = const.tile([P, HD], BF16, name="cosb")
        sinb = const.tile([P, HD], BF16, name="sinb")
        nc.scalar.dma_start(out=sinb[:], in_=sin.flatten_outer_dims())
        nc.scalar.dma_start(out=cosb[:], in_=cos.flatten_outer_dims())
        nc.scalar.dma_start(out=brows[0:4, :], in_=bk.rearrange("(f n) -> f n", n=N_TILE))
        scratch = const.tile([P, 1], F32, name="scratch")
        nc.scalar.copy(out=scratch[:], in_=warm[:, 0:1])

        xraw = []

        def load_x(m):
            xt = rawp.tile([P, DIM], BF16, name="raw", tag="raw")
            pieces = 2 if m == 0 else 1
            w = DIM // pieces
            for q in range(pieces):
                nc.sync.dma_start(out=xt[:, q * w:(q + 1) * w], in_=xf[m * P:(m + 1) * P, q * w:(q + 1) * w])
            xraw.append(xt)

        load_x(0)
        load_x(1)

        wtiles = {}

        def load_ft(i):
            which, f = FT_ORDER[i]
            src = wk if which == "k" else wv
            tiles = []
            if i < KHALF_FTS:
                for kh in range(2):
                    for pair in range(2):
                        wt = rawp.tile([P, DIM], BF16, name="raw", tag="raw")
                        r0 = f * N_TILE + pair * 2 * P
                        nc.sync.dma_start(
                            out=wt[:].rearrange("p (r k) -> p r k", r=2),
                            in_=src[r0:r0 + 2 * P, kh * 1024:(kh + 1) * 1024].rearrange("(r p) k -> p r k", p=P),
                        )
                        tiles.append(wt)
            else:
                for rb in range(4):
                    wt = rawp.tile([P, DIM], BF16, name="raw", tag="raw")
                    r0 = f * N_TILE + rb * P
                    nc.sync.dma_start(out=wt[:], in_=src[r0:r0 + P, :])
                    tiles.append(wt)
            wtiles[i] = tiles

        def run_words(r, rb):
            i, kh = divmod(r, 2)
            if i < KHALF_FTS:
                wt = wtiles[i][kh * 2 + rb // 2]
                base = (rb % 2) * 512
            else:
                wt = wtiles[i][rb]
                base = kh * 512
            return wt[:].bitcast(F32)[:, base:base + 512]

        load_ft(0)
        load_x(2)
        load_x(3)
        for i in range(1, 4):
            load_ft(i)

        bk_late = const.tile([P, E - N_BIAS_MM * N_TILE], BF16, name="bk_late")
        nc.sync.dma_start(out=bk_late[:], in_=bk[N_BIAS_MM * N_TILE:E].partition_broadcast(P))
        bv_all = const.tile([P, E], BF16, name="bv_all")
        nc.sync.dma_start(out=bv_all[:], in_=bv.partition_broadcast(P))

        tabsrc = const.tile([P, 2 * HD], BF16, name="tabsrc")
        nc.vector.tensor_copy(out=tabsrc[:, 0:64], in_=cosb[:, 0:64])
        nc.vector.tensor_copy(out=tabsrc[:, 64:128], in_=sinb[:, 64:128])
        nc.vector.tensor_scalar(out=tabsrc[:, 128:192], in0=sinb[:, 0:64], scalar1=-1.0, scalar2=None, op0=MULT)
        nc.vector.tensor_copy(out=tabsrc[:, 192:256], in_=cosb[:, 64:128])

        def word_rows(g, lo, hi):
            return g[:].bitcast(F32).rearrange("p (r u) -> p r u", u=2)[:, lo:hi, :]

        def bank_out(bank):
            return bank[:].rearrange("p u r -> p r u")

        bias = {}

        def bias_mm(i, engine):
            which, f = FT_ORDER[i]
            row = f if which == "k" else 4 + f
            ps = bankp.tile([P, N_TILE], F32, name="bank", tag="bank")
            nc.tensor.matmul(out=ps[:], lhsT=identb[:, row:row + 1].to_broadcast([P, P]), rhs=brows[:], start=True, stop=True)
            bt = const.tile([P, N_TILE], BF16, name="bias%d" % i)
            if engine == "s":
                nc.scalar.copy(out=bt[:], in_=ps[:])
            else:
                nc.vector.tensor_copy(out=bt[:], in_=ps[:])
            bias[i] = bt[:]

        xg = {}
        xcodes = {}
        xscales = {}

        def t_run_x(half):
            g = grp.tile([P, 2 * DIM], BF16, name="grouped", tag="grouped", align_bytes=64)
            for ml in range(2):
                words = xraw[2 * half + ml][:].bitcast(F32)
                for ch in range(2):
                    bank = bankp.tile([P, 2, 256], F32, name="bank", tag="bank")
                    for cl in range(2):
                        c = 2 * ch + cl
                        for u in range(2):
                            nc.tensor.transpose(bank[:, u, cl * P:(cl + 1) * P], words[:, c * 256 + u:(c + 1) * 256:2], ident[:])
                    lo = ml * 512 + ch * 256
                    if ch == 0:
                        nc.scalar.copy(out=word_rows(g, lo, lo + 256), in_=bank_out(bank))
                    else:
                        nc.vector.tensor_copy(out=word_rows(g, lo, lo + 256), in_=bank_out(bank))
            xg[half] = g

        def quant_x(half):
            xc = const.tile([P, 2 * N_TILE], U32, name="xcodes%d" % half, align_bytes=64)
            xs = const.tile([P, 2 * N_TILE], U8, name="xscales%d" % half, align_bytes=64)
            nc.vector.quantize_mx(out=xc[:].bitcast(FP8X4), scales=xs[:], in_=xg[half][:])
            xcodes[half] = xc
            xscales[half] = xs

        wg = {}
        wcodes = {}
        wscales = {}
        reord = {}

        v_reorders = []

        def reorder_run(r):
            for rb in REORD_RBS:
                ro = rop.tile([P, 512], F32, name="ro", tag="ro")
                reord[(r, rb)] = ro
                if r == FIRST_REORD_RUN:
                    v_reorders.append((r, rb))
                    continue
                nc.scalar.copy(
                    out=ro[:].rearrange("p (c u q) -> p c q u", c=2, u=2),
                    in_=run_words(r, rb).rearrange("p (c q u) -> p c q u", c=2, u=2),
                )

        def reorder_on_vector():
            for r, rb in v_reorders:
                nc.vector.tensor_copy(
                    out=reord[(r, rb)][:].rearrange("p (c u q) -> p c q u", c=2, u=2),
                    in_=run_words(r, rb).rearrange("p (c q u) -> p c q u", c=2, u=2),
                )
            v_reorders.clear()

        def t_run_w(r):
            g = grp.tile([P, 2 * DIM], BF16, name="grouped", tag="grouped", align_bytes=64)
            for pair in range(2):
                for cl in range(2):
                    bank = bankp.tile([P, 2, 256], F32, name="bank", tag="bank")
                    for rl in range(2):
                        rb = 2 * pair + rl
                        for u in range(2):
                            if (r, rb) in reord:
                                src = reord[(r, rb)][:, cl * 256 + u * P:cl * 256 + (u + 1) * P]
                            else:
                                src = run_words(r, rb)[:, cl * 256 + u:(cl + 1) * 256:2]
                            nc.tensor.transpose(bank[:, u, rl * P:(rl + 1) * P], src, ident[:])
                    lo = cl * 512 + pair * 256
                    nc.scalar.copy(out=word_rows(g, lo, lo + 256), in_=bank_out(bank))
            wg[r] = g

        def quant_w(r):
            wc = codep.tile([P, 2 * N_TILE], U32, name="wcodes", tag="wcodes", align_bytes=64)
            ws = codep.tile([P, 2 * N_TILE], U8, name="wscales", tag="wscales", align_bytes=64)
            nc.vector.quantize_mx(out=wc[:].bitcast(FP8X4), scales=ws[:], in_=wg[r][:])
            wcodes[r] = wc
            wscales[r] = ws

        accs = {}

        def m_group(i, m):
            acc = bankp.tile([P, N_TILE], F32, name="bank", tag="bank")
            for c in range(4):
                r = 2 * i + c // 2
                wcol = slice((c % 2) * N_TILE, (c % 2 + 1) * N_TILE)
                xcol = slice((m % 2) * N_TILE + c * P, (m % 2) * N_TILE + (c + 1) * P)
                nc.tensor.matmul_mx(
                    out=acc[:],
                    lhsT=xcodes[m // 2][:, xcol].bitcast(FP8X4),
                    lhsT_scale=xscales[m // 2][:, xcol],
                    rhs=wcodes[r][:, wcol].bitcast(FP8X4),
                    rhs_scale=wscales[r][:, wcol],
                    start=(c == 0),
                    stop=(c == 3),
                )
            accs[(i, m)] = acc

        def bank_heads(ap):
            return ap.rearrange("p (h d) -> p h d", d=HD)

        tab = tabp.tile([P, 2, 2, 64], F32, name="tab")
        gdep = const.tile([P, 1], U32, name="gdep")
        jobs = []
        unsent = []
        job_state = {"next": 0, "cur": None}

        def read_k(i, ms):
            for m in ms:
                t = kep.tile([P, N_TILE], F32, name="t", tag="t", bufs=8)
                nc.vector.tensor_tensor(out=t[:], in0=accs[(i, m)][:], in1=bias[i], op=ADD)
                jobs.append({"t": t, "m": m, "f": FT_ORDER[i][1]})

        def pre_job():
            if job_state["next"] == len(jobs):
                return
            job = jobs[job_state["next"]]
            job_state["next"] += 1
            job_state["cur"] = job
            ab = kep.tile([P, 2 * N_TILE], F32, name="ab", tag="ab", bufs=3)
            job["ab"] = ab
            nh = HEADS_PER_TILE
            nc.vector.tensor_tensor(
                out=ab[:].rearrange("p (h s y d) -> p h s y d", s=2, y=2, d=64),
                in0=job["t"][:].rearrange("p (h s d) -> p h s d", s=2, d=64).unsqueeze(3).to_broadcast([P, nh, 2, 2, 64]),
                in1=tab[:].unsqueeze(1).to_broadcast([P, nh, 2, 2, 64]),
                op=MULT,
            )

        def post_job(after_quant):
            job = job_state["cur"]
            if job is None:
                return
            job_state["cur"] = None
            if after_quant is not None:
                nc.gpsimd.tensor_copy(out=gdep[:], in_=wcodes[after_quant][:, 0:1])
            a = kep.tile([P, N_TILE], F32, name="a", tag="a", bufs=12)
            job["a"] = a
            abv = job["ab"][:].rearrange("p (h s e) -> p h s e", s=2, e=HD)
            nc.gpsimd.tensor_tensor(out=bank_heads(a[:]), in0=abv[:, :, 0, :], in1=abv[:, :, 1, :], op=ADD)
            unsent.append(job)

        def send_k():
            for job in unsent:
                f = job["f"]
                nc.sync.dma_start(
                    out=out_0[job["m"], f * HEADS_PER_TILE:(f + 1) * HEADS_PER_TILE, :, :].rearrange("h s d -> s h d"),
                    in_=bank_heads(job["a"][:]),
                )
            unsent.clear()

        def read_v(i, ms):
            f = FT_ORDER[i][1]
            for m in ms:
                vout = vep.tile([P, N_TILE], F32, name="vout", tag="vout")
                pieces = 1
                if i == len(FT_ORDER) - 1 and m == B - 1:
                    pieces = 4
                if i == len(FT_ORDER) - 1 and m == B - 2:
                    pieces = 2
                hp = HEADS_PER_TILE // pieces
                for q in range(pieces):
                    cols = slice(q * hp * HD, (q + 1) * hp * HD)
                    nc.vector.tensor_tensor(out=vout[:, cols], in0=accs[(i, m)][:, cols], in1=bias[i][:, cols], op=ADD)
                    h0 = f * HEADS_PER_TILE + q * hp
                    nc.sync.dma_start(
                        out=out_1[m, h0:h0 + hp, :, :].rearrange("h s d -> s h d"),
                        in_=vout[:, cols].rearrange("p (h d) -> p h d", d=HD),
                    )

        for i in range(N_BIAS_MM, len(FT_ORDER)):
            which, f = FT_ORDER[i]
            if which == "k":
                bias[i] = bk_late[:, (f - N_BIAS_MM) * N_TILE:(f - N_BIAS_MM + 1) * N_TILE]
            else:
                bias[i] = bv_all[:, f * N_TILE:(f + 1) * N_TILE]

        wps = bankp.tile([P, N_TILE], F32, name="bank", tag="bank")
        for n in range(N_WARM):
            nc.tensor.matmul(out=wps[:], lhsT=warm[:, 0:P], rhs=warm[:], start=True, stop=True)

        t_run_x(0)
        quant_x(0)
        t_run_w(0)
        quant_w(0)
        t_run_w(1)
        nc.tensor.matmul(out=tab[:].rearrange("p s y d -> p (s y d)"), lhsT=identb[:], rhs=tabsrc[:], start=True, stop=True)
        quant_w(1)
        bias_mm(0, "s")
        bias_mm(1, "v")
        t_run_x(1)
        quant_x(1)
        load_ft(4)
        load_ft(5)

        reord_state = {"next": FIRST_REORD_RUN}

        def products(p):
            i = p // 2
            ms = (2 * (p % 2), 2 * (p % 2) + 1)
            for m in ms:
                m_group(i, m)
            if FT_ORDER[i][0] == "k":
                read_k(i, ms)
            else:
                read_v(i, ms)

        for p in range(n_runs):
            if p == 0:
                m_group(0, 0)
                read_k(0, (0,))
            if p + 2 < n_runs:
                t_run_w(p + 2)
            while reord_state["next"] < min(n_runs, p + (REORD_AHEAD if p == 0 else REORD_AHEAD + 1)):
                reorder_run(reord_state["next"])
                reord_state["next"] += 1
            if p == 1:
                load_ft(6)
            if p == 3:
                load_ft(7)
            send_k()
            pre_job()
            reorder_on_vector()
            if p + 2 < n_runs:
                quant_w(p + 2)
            post_job(p + 2 if p + 2 < n_runs else None)
            if p in TWO_JOB_PERIODS:
                pre_job()
                post_job(None)
            if p == 0:
                m_group(0, 1)
                read_k(0, (1,))
            else:
                products(p)
        assert job_state["next"] == len(jobs) and job_state["cur"] is None and not unsent
